import numpy as np
import ml_dtypes


def mxq(x, axis, fmt="e4m3"):
    dtype, down = {"e4m3": (ml_dtypes.float8_e4m3fn, 7), "e5m2": (ml_dtypes.float8_e5m2, 14)}[fmt]
    v = np.moveaxis(np.asarray(x, np.float32).astype(ml_dtypes.bfloat16).astype(np.float64), axis, -1)
    blocks = v.reshape(v.shape[:-1] + (-1, 32))
    amax = np.abs(blocks).max(-1, keepdims=True)
    byte = np.maximum(np.where(amax > 0, np.frexp(amax)[1] - 1 + 127, 0) - down, 1)
    scale = np.exp2(byte - 127.0)
    codes = (blocks / scale).astype(np.float32).astype(dtype).astype(np.float64)
    return np.moveaxis((codes * scale).reshape(v.shape), -1, axis)


WIDE = False


def mx_kscale(k):
    if not WIDE:
        return np.ones(k)
    levels = np.array([10, -10, 5, -5, 0])
    a = np.random.permutation(np.resize(levels, k // 512 * 4)).reshape(k // 512, 4)
    idx = np.arange(k)
    return np.exp2(a[idx // 512, idx % 128 // 32])


BF16 = ml_dtypes.bfloat16


def bf(x):
    return np.asarray(x, np.float32).astype(BF16)


def f64(x):
    return np.asarray(x).astype(np.float64)


B, H, N, DK, DF, R = 1, 8, 512, 1025, 128, 4
LAG = 1
EPS = 1e-6
T = DK - LAG


def mix(w, z):
    return sum(w[..., r:r + 1] * z[:, :, r:r + 1, :] for r in range(R))


def setup_inputs():
    z = np.random.standard_normal((B, H, R, DK + LAG))
    a = np.random.standard_normal((B, H, N, R)) / np.sqrt(R)
    c = np.random.standard_normal((B, H, N, R)) / np.sqrt(R)
    q = mix(a, z[..., LAG:]) + 0.5 * np.random.standard_normal((B, H, N, DK)) + 0.5 * np.random.standard_normal((B, H, N, 1))
    k = mix(c, z[..., :DK]) + 0.5 * np.random.standard_normal((B, H, N, DK)) + 0.5 * np.random.standard_normal((B, H, N, 1))
    s = mx_kscale(N)
    g = (s / s.min())[:, None]
    return {"q_t": bf(0.6 * q * g), "k_t": bf(0.6 * k * g)}


def reference(q_t, k_t):
    xp = f64(q_t)[..., :T]
    yf = f64(k_t)[..., LAG:]
    xp = xp - xp.mean(-1, keepdims=True)
    yf = yf - yf.mean(-1, keepdims=True)
    cov = (mxq(xp, 3, "e4m3") @ mxq(yf.transpose(0, 1, 3, 2), 2, "e4m3")) / T
    vx = np.mean(xp * xp, axis=-1)
    vy = np.mean(yf * yf, axis=-1)
    rho2 = (cov * cov) / (vx[..., :, None] * vy[..., None, :] + EPS)
    return -0.5 * np.log(1.0 - rho2 + EPS)

@@ -1,0 +1,363 @@
+from contextlib import ExitStack
+
+import concourse.mybir as mybir
+from concourse.masks import make_identity
+
+F32 = mybir.dt.float32
+BF16 = mybir.dt.bfloat16
+U32 = mybir.dt.uint32
+U8 = mybir.dt.uint8
+FP8X4 = mybir.dt.float8_e4m3fn_x4
+ALU = mybir.AluOpType
+ACT = mybir.ActivationFunctionType
+AX = mybir.AxisListType
+
+H = 8
+NS = 512
+T = 1024
+P = 128
+SER = 32
+CH = 4
+CW = 256
+NT = 16
+EPS = 1e-6
+NBL = [4, 4, 4, 4, 4, 4, 4, 4]
+W7_ON = "GGGGGGGG"
+W9_ON = "GGGGGGGG"
+TBUFS = 3
+FLOPS = 2 * H * NS * NS * T
+
+
+def tile_entropygraph_pa_t_kernel(tc, q_t, k_t, out):
+    nc = tc.nc
+    with ExitStack() as ctx:
+        const = ctx.enter_context(tc.tile_pool(name="const", bufs=1))
+        rawp = ctx.enter_context(tc.tile_pool(name="rawp", bufs=3))
+        xcp = ctx.enter_context(tc.tile_pool(name="xcp", bufs=2))
+        grpp = ctx.enter_context(tc.tile_pool(name="grpp", bufs=2))
+        cdp = ctx.enter_context(tc.tile_pool(name="cdp", bufs=2))
+        statp = ctx.enter_context(tc.tile_pool(name="statp", bufs=2))
+        sp = ctx.enter_context(tc.tile_pool(name="sp", bufs=2))
+        tpl = ctx.enter_context(tc.tile_pool(name="tpl", bufs=TBUFS))
+        tpp = ctx.enter_context(tc.psum_pool(name="tpp", bufs=2))
+        accp = ctx.enter_context(tc.psum_pool(name="accp", bufs=4))
+        stp = ctx.enter_context(tc.psum_pool(name="stp", bufs=1))
+
+        ident_f = const.tile([P, P], F32, name="ident_f")
+        make_identity(nc, ident_f[:])
+        ident_b = const.tile([P, P], BF16, name="ident_b")
+        nc.vector.tensor_copy(out=ident_b[:], in_=ident_f[:])
+        mask = const.tile([P, SER], F32, name="mask")
+        nc.vector.tensor_reduce(out=mask[:], in_=ident_f[:].rearrange("p (i j) -> p i j", j=CH), axis=AX.X, op=ALU.add)
+        quad = const.tile([P, 4], F32, name="quad")
+        nc.vector.tensor_reduce(out=quad[:], in_=ident_f[:].rearrange("p (a i) -> p a i", i=SER), axis=AX.X, op=ALU.add)
+        bneg = const.tile([P, SER, CH], F32, name="bneg")
+        nc.vector.tensor_scalar(
+            out=bneg[:], in0=mask[:].unsqueeze(2).to_broadcast([P, SER, CH]), scalar1=-0.125, scalar2=None, op0=ALU.mult
+        )
+        brep = const.tile([P, 4, SER], F32, name="brep")
+        nc.vector.tensor_scalar(
+            out=brep[:], in0=mask[:].unsqueeze(1).to_broadcast([P, 4, SER]), scalar1=1.0 / T, scalar2=None, op0=ALU.mult
+        )
+        one = const.tile([P, 1], F32, name="one")
+        nc.vector.memset(one[:], 1.0)
+        c1 = const.tile([P, 1], F32, name="c1")
+        nc.vector.tensor_scalar(out=c1[:], in0=one[:], scalar1=EPS, scalar2=None, op0=ALU.add)
+        cst = const.tile([P, 2, 4], F32, name="cst")
+        nc.vector.tensor_scalar(out=cst[:, 0, :], in0=one[:].to_broadcast([P, 4]), scalar1=EPS, scalar2=None, op0=ALU.mult)
+        nc.vector.tensor_scalar(out=cst[:, 1, :], in0=one[:].to_broadcast([P, 4]), scalar1=-1.0 / (T * T), scalar2=None, op0=ALU.mult)
+        junk = const.tile([P, CW], BF16, name="junk")
+        bnegv = bneg[:].rearrange("p i j -> p (i j)")
+        brepv = brep[:].rearrange("p a i -> p (a i)")
+
+        hd = [dict() for h in range(H)]
+
+        def ok(h):
+            return 0 <= h < H
+
+        def load(h):
+            raw = rawp.tile([P, 2, NT, CW], BF16, name="raw")
+            hd[h]["raw"] = raw
+            cuts = ((0, 4), (4, NT)) if h == 0 else ((0, NT),)
+            for o in range(2):
+                src = (q_t, k_t)[o]
+                for a0, a1 in cuts:
+                    for j in range(CH):
+                        lo = o + j * CW
+                        nc.sync.dma_start(
+                            out=raw[j:P:CH, o, a0:a1, :],
+                            in_=src[0, h, SER * a0 : SER * a1, lo : lo + CW].rearrange("(a i) k -> i a k", i=SER),
+                        )
+
+        def bsum(h, b):
+            nb = NBL[h]
+            if b == 0:
+                hd[h]["sms"] = statp.tile([P, NT], F32, name="sms")
+            nc.scalar.activation(
+                out=junk[:],
+                in_=hd[h]["raw"][:, 1, NT - nb + b, :],
+                func=ACT.Copy,
+                scale=1.0 / 128.0,
+                accum_out=hd[h]["sms"][:, b : b + 1],
+            )
+
+        def bn(h):
+            nat = 2 * NT - NBL[h]
+            raw = hd[h]["raw"]
+            st = statp.tile([P, 2 * NT, 6], F32, name="st")
+            hd[h]["st"] = st
+            for c in range(nat):
+                nc.vector.bn_stats(out=st[:, c, :], in_=raw[:, c // NT, c % NT, :])
+            smv = statp.tile([P, 2 * NT], F32, name="smv")
+            hd[h]["smv"] = smv
+            stv = st[:].rearrange("p t (e f) -> p t e f", f=3)
+            nc.vector.tensor_reduce(out=smv[:, 0:nat], in_=stv[:, 0:nat, :, 1], axis=AX.X, op=ALU.add)
+
+        def ms(h):
+            nat = 2 * NT - NBL[h]
+            sta = stp.tile([P, 2 * NT], F32, name="sta")
+            hd[h]["sta"] = sta
+            nc.tensor.matmul(out=sta[:, 0:nat], lhsT=bnegv, rhs=hd[h]["smv"][:, 0:nat], start=True, stop=True)
+            if NBL[h]:
+                nc.tensor.matmul(out=sta[:, nat : 2 * NT], lhsT=bnegv, rhs=hd[h]["sms"][:, 0 : NBL[h]], start=True, stop=True)
+
+        def centre(h, extra):
+            nat = 2 * NT - NBL[h]
+            raw = hd[h]["raw"]
+            negm = statp.tile([P, 2 * NT], F32, name="negm")
+            hd[h]["negm"] = negm
+            nc.vector.tensor_copy(out=negm[:], in_=hd[h]["sta"][:])
+            xc = xcp.tile([P, 2, NT, CW], BF16, name="xc")
+            hd[h]["xc"] = xc
+            stv = hd[h]["st"][:].rearrange("p t (e f) -> p t e f", f=3)
+            dd = statp.tile([P, 2 * NT, 2], F32, name="dd")
+            ptv = statp.tile([P, 2 * NT], F32, name="ptv")
+            hd[h]["ptv"] = ptv
+
+            def some(lo, hi):
+                for c in range(lo, hi):
+                    nc.vector.tensor_scalar(
+                        out=xc[:, c // NT, c % NT, :],
+                        in0=raw[:, c // NT, c % NT, :],
+                        scalar1=negm[:, c : c + 1],
+                        scalar2=None,
+                        op0=ALU.add,
+                    )
+
+            small = [
+                lambda: nc.vector.tensor_tensor(
+                    out=dd[:, 0:nat, :],
+                    in0=stv[:, 0:nat, :, 1],
+                    in1=negm[:, 0:nat].unsqueeze(2).to_broadcast([P, nat, 2]),
+                    op=ALU.add,
+                ),
+                lambda: nc.vector.tensor_tensor(out=dd[:, 0:nat, :], in0=dd[:, 0:nat, :], in1=dd[:, 0:nat, :], op=ALU.mult),
+                lambda: nc.vector.scalar_tensor_tensor(
+                    out=dd[:, 0:nat, :], in0=dd[:, 0:nat, :], scalar=128.0, in1=stv[:, 0:nat, :, 2], op0=ALU.mult, op1=ALU.add
+                ),
+                lambda: nc.vector.tensor_reduce(out=ptv[:, 0:nat], in_=dd[:, 0:nat, :], axis=AX.X, op=ALU.add),
+            ]
+            both = []
+            for n in range(max(len(small), len(extra))):
+                both.extend(extra[n : n + 1])
+                both.extend(small[n : n + 1])
+            for n in range(NT):
+                some(2 * n, 2 * n + 2)
+                if n < len(both):
+                    both[n]()
+
+        def bsq(h):
+            nb = NBL[h]
+            raw = hd[h]["raw"]
+            negm = hd[h]["negm"]
+            pts = statp.tile([P, NT], F32, name="pts")
+            hd[h]["pts"] = pts
+            for b in range(nb):
+                c = 2 * NT - nb + b
+                nc.scalar.activation(
+                    out=junk[:],
+                    in_=raw[:, 1, NT - nb + b, :],
+                    func=ACT.Square,
+                    bias=negm[:, c : c + 1],
+                    scale=1.0,
+                    accum_out=pts[:, b : b + 1],
+                )
+
+        def tot(h):
+            nat = 2 * NT - NBL[h]
+            stt = stp.tile([P, 2 * NT], F32, name="sta")
+            hd[h]["stt"] = stt
+            nc.tensor.matmul(out=stt[:, 0:nat], lhsT=brepv, rhs=hd[h]["ptv"][:, 0:nat], start=True, stop=True)
+            if NBL[h]:
+                nc.tensor.matmul(out=stt[:, nat : 2 * NT], lhsT=brepv, rhs=hd[h]["pts"][:, 0 : NBL[h]], start=True, stop=True)
+
+        def sel(h):
+            tmp = statp.tile([P, 8, 4], F32, name="tmp")
+            var = statp.tile([P, 8], F32, name="var")
+            kap = statp.tile([P, 4], F32, name="kap")
+            sc = statp.tile([P, 4], F32, name="sc")
+            bl = statp.tile([P, 2, 4], F32, name="bl")
+            hd[h]["var"] = var
+            hd[h]["sc"] = sc
+            hd[h]["bl"] = bl
+            nc.vector.tensor_tensor(
+                out=tmp[:],
+                in0=hd[h]["stt"][:].rearrange("p (b a) -> p b a", a=4),
+                in1=quad[:].unsqueeze(1).to_broadcast([P, 8, 4]),
+                op=ALU.mult,
+            )
+            return [
+                lambda: nc.vector.tensor_reduce(out=var[:], in_=tmp[:], axis=AX.X, op=ALU.add),
+                lambda: nc.vector.tensor_scalar(out=kap[:], in0=var[:, 0:4], scalar1=EPS, scalar2=None, op0=ALU.max),
+                lambda: nc.vector.reciprocal(out=kap[:], in_=kap[:]),
+                lambda: nc.vector.tensor_tensor(out=sc[:], in0=kap[:], in1=var[:, 0:4], op=ALU.mult),
+                lambda: nc.vector.tensor_tensor(out=bl[:], in0=kap[:].unsqueeze(1).to_broadcast([P, 2, 4]), in1=cst[:], op=ALU.mult),
+            ]
+
+        def bcast(h):
+            stb = stp.tile([P, NS], F32, name="stb")
+            hd[h]["stb"] = stb
+            for nt in range(4):
+                nc.tensor.matmul(
+                    out=stb[:, P * nt : P * (nt + 1)],
+                    lhsT=hd[h]["var"][:, 4 + nt : 5 + nt].to_broadcast([P, P]),
+                    rhs=ident_f[:],
+                    start=True,
+                    stop=True,
+                )
+
+        def rsq(h):
+            s = sp.tile([P, 4, NS], F32, name="s")
+            hd[h]["s"] = s
+            for mt in range(4):
+                nc.scalar.activation(
+                    out=s[:, mt, :],
+                    in_=hd[h]["stb"][:],
+                    func=ACT.Abs_reciprocal_sqrt,
+                    bias=hd[h]["bl"][:, 0, mt : mt + 1],
+                    scale=hd[h]["sc"][:, mt : mt + 1],
+                )
+
+        def tco(h):
+            xc = hd[h]["xc"]
+            grp = grpp.tile([P, 2, 2, 2048], BF16, name="grp", align_bytes=64)
+            hd[h]["grp"] = grp
+            for g in range(2):
+                for o in range(2):
+                    for b in range(2):
+                        tp = tpp.tile([P, 1024], BF16, name="tp")
+                        for u in range(8):
+                            nc.tensor.transpose(tp[:, P * u : P * (u + 1)], xc[:, o, 8 * b + u, P * g : P * (g + 1)], ident_b[:])
+                        nc.scalar.copy(out=grp[:, g, o, 1024 * b : 1024 * (b + 1)], in_=tp[:])
+                        n = 4 * g + 2 * o + b
+                        if ok(h + 1) and n < NBL[h + 1]:
+                            bsum(h + 1, n)
+
+        def quant(h):
+            grp = hd[h]["grp"]
+            codes = cdp.tile([P, 2, 2, NS], U32, name="codes", align_bytes=64)
+            scl = cdp.tile([P, 2, 2, NS], U8, name="scl", align_bytes=64)
+            hd[h]["codes"] = codes
+            hd[h]["scl"] = scl
+            for g in range(2):
+                for o in range(2):
+                    nc.vector.quantize_mx(out=codes[:, g, o, :].bitcast(FP8X4), scales=scl[:, g, o, :], in_=grp[:, g, o, :])
+
+        def mx(h):
+            codes = hd[h]["codes"]
+            scl = hd[h]["scl"]
+            accs = [accp.tile([P, NS], F32, name="acc") for mt in range(4)]
+            hd[h]["acc"] = accs
+            for g in range(2):
+                for mt in range(4):
+                    nc.tensor.matmul_mx(
+                        out=accs[mt][:],
+                        lhsT=codes[:, g, 0, P * mt : P * (mt + 1)].bitcast(FP8X4),
+                        lhsT_scale=scl[:, g, 0, P * mt : P * (mt + 1)],
+                        rhs=codes[:, g, 1, :].bitcast(FP8X4),
+                        rhs_scale=scl[:, g, 1, :],
+                        start=(g == 0),
+                        stop=(g == 1),
+                    )
+
+        def w6(h):
+            t = tpl.tile([P, 4, NS], F32, name="t")
+            hd[h]["t"] = t
+            for mt in range(4):
+                nc.vector.tensor_tensor(out=t[:, mt, :], in0=hd[h]["acc"][mt][:], in1=hd[h]["s"][:, mt, :], op=ALU.mult)
+
+        def w7(h):
+            t = hd[h]["t"]
+            for mt in range(4):
+                if W7_ON[h] == "G":
+                    nc.gpsimd.tensor_tensor(out=t[:, mt, :], in0=t[:, mt, :], in1=t[:, mt, :], op=ALU.mult)
+                else:
+                    nc.scalar.activation(out=t[:, mt, :], in_=t[:, mt, :], func=ACT.Square)
+
+        def ln(h):
+            t = hd[h]["t"]
+            for mt in range(4):
+                nc.scalar.activation(out=t[:, mt, :], in_=t[:, mt, :], func=ACT.Ln, bias=c1[:], scale=hd[h]["bl"][:, 1, mt : mt + 1])
+
+        def w9(h):
+            t = hd[h]["t"]
+            ov = out[0, h, :, :].rearrange("(mt m) j -> m mt j", m=P)
+            for half in range(2):
+                sl = t[:, 2 * half : 2 * half + 2, :]
+                if W9_ON[h] == "V":
+                    nc.vector.tensor_scalar(out=sl, in0=sl, scalar1=-0.5, scalar2=None, op0=ALU.mult)
+                elif W9_ON[h] == "S":
+                    nc.scalar.activation(out=sl, in_=sl, func=ACT.Copy, scale=-0.5)
+                else:
+                    nc.gpsimd.tensor_scalar(out=sl, in0=sl, scalar1=-0.5, scalar2=0.0, op0=ALU.mult, op1=ALU.add)
+                nc.sync.dma_start(out=ov[:, 2 * half : 2 * half + 2, :], in_=sl)
+
+        with tc.manual_schedule():
+            for h in range(3):
+                load(h)
+            done = {"ln": 0, "w9": 0}
+
+            def logs(upto):
+                while done["ln"] < min(upto, H):
+                    ln(done["ln"])
+                    done["ln"] += 1
+
+            def halves(most):
+                n = 0
+                while done["w9"] < done["ln"] and n < most:
+                    w9(done["w9"])
+                    done["w9"] += 1
+                    n += 1
+
+            for b in range(NBL[0]):
+                bsum(0, b)
+            for i in range(-2, H + 1):
+                if i >= -1 and ok(i + 4):
+                    load(i + 4)
+                if ok(i - 1):
+                    w6(i - 1)
+                    w7(i - 1)
+                halves(H)
+                if ok(i + 1):
+                    bsq(i + 1)
+                    tco(i + 1)
+                    tot(i + 1)
+                if ok(i):
+                    rsq(i)
+                logs(i)
+                if ok(i + 2):
+                    bn(i + 2)
+                extra = sel(i + 1) if ok(i + 1) else []
+                if ok(i + 2):
+                    ms(i + 2)
+                if ok(i):
+                    quant(i)
+                    mx(i)
+                if ok(i + 2):
+                    centre(i + 2, extra)
+                else:
+                    for op in extra:
+                        op()
+                if ok(i + 1):
+                    bcast(i + 1)
+            halves(H)

@@ -21,6 +21,8 @@ CH = 4
 CW = 256
 NT = 16
 EPS = 1e-6
+SC0 = 32
+SW = 40
 NBL = [4, 4, 4, 4, 4, 4, 4, 4]
 W7_ON = "GGGGGGGG"
 W9_ON = "GGGGGGGG"
@@ -39,8 +41,7 @@ def tile_entropygraph_pa_t_kernel(tc, q_t, k_t, out):
         statp = ctx.enter_context(tc.tile_pool(name="statp", bufs=2))
         sp = ctx.enter_context(tc.tile_pool(name="sp", bufs=2))
         tpl = ctx.enter_context(tc.tile_pool(name="tpl", bufs=TBUFS))
-        tpp = ctx.enter_context(tc.psum_pool(name="tpp", bufs=2))
-        accp = ctx.enter_context(tc.psum_pool(name="accp", bufs=4))
+        bank = ctx.enter_context(tc.psum_pool(name="bank", bufs=6))
         stp = ctx.enter_context(tc.psum_pool(name="stp", bufs=1))
 
         ident_f = const.tile([P, P], F32, name="ident_f")
@@ -70,7 +71,16 @@ def tile_entropygraph_pa_t_kernel(tc, q_t, k_t, out):
         bnegv = bneg[:].rearrange("p i j -> p (i j)")
         brepv = brep[:].rearrange("p a i -> p (a i)")
 
+        smt = [const.tile([P, SW], F32, name="smt%d" % n) for n in range(2)]
+        ptt = [const.tile([P, SW], F32, name="ptt%d" % n) for n in range(2)]
+        for n in range(2):
+            nc.vector.memset(smt[n][:], 0.0)
+            nc.vector.memset(ptt[n][:], 0.0)
+
         hd = [dict() for h in range(H)]
+
+        def col(h, c):
+            return c if c < 2 * NT - NBL[h] else SC0 + c - (2 * NT - NBL[h])
 
         def ok(h):
             return 0 <= h < H
@@ -91,14 +101,12 @@ def tile_entropygraph_pa_t_kernel(tc, q_t, k_t, out):
 
         def bsum(h, b):
             nb = NBL[h]
-            if b == 0:
-                hd[h]["sms"] = statp.tile([P, NT], F32, name="sms")
             nc.scalar.activation(
                 out=junk[:],
                 in_=hd[h]["raw"][:, 1, NT - nb + b, :],
                 func=ACT.Copy,
                 scale=1.0 / 128.0,
-                accum_out=hd[h]["sms"][:, b : b + 1],
+                accum_out=smt[h % 2][:, SC0 + b : SC0 + b + 1],
             )
 
         def bn(h):
@@ -108,38 +116,32 @@ def tile_entropygraph_pa_t_kernel(tc, q_t, k_t, out):
             hd[h]["st"] = st
             for c in range(nat):
                 nc.vector.bn_stats(out=st[:, c, :], in_=raw[:, c // NT, c % NT, :])
-            smv = statp.tile([P, 2 * NT], F32, name="smv")
-            hd[h]["smv"] = smv
             stv = st[:].rearrange("p t (e f) -> p t e f", f=3)
-            nc.vector.tensor_reduce(out=smv[:, 0:nat], in_=stv[:, 0:nat, :, 1], axis=AX.X, op=ALU.add)
+            nc.vector.tensor_reduce(out=smt[h % 2][:, 0:nat], in_=stv[:, 0:nat, :, 1], axis=AX.X, op=ALU.add)
 
         def ms(h):
-            nat = 2 * NT - NBL[h]
-            sta = stp.tile([P, 2 * NT], F32, name="sta")
+            sta = stp.tile([P, SW], F32, name="sta")
             hd[h]["sta"] = sta
-            nc.tensor.matmul(out=sta[:, 0:nat], lhsT=bnegv, rhs=hd[h]["smv"][:, 0:nat], start=True, stop=True)
-            if NBL[h]:
-                nc.tensor.matmul(out=sta[:, nat : 2 * NT], lhsT=bnegv, rhs=hd[h]["sms"][:, 0 : NBL[h]], start=True, stop=True)
+            nc.tensor.matmul(out=sta[:], lhsT=bnegv, rhs=smt[h % 2][:], start=True, stop=True)
 
         def centre(h, extra):
             nat = 2 * NT - NBL[h]
             raw = hd[h]["raw"]
-            negm = statp.tile([P, 2 * NT], F32, name="negm")
+            negm = statp.tile([P, SW], F32, name="negm")
             hd[h]["negm"] = negm
             nc.vector.tensor_copy(out=negm[:], in_=hd[h]["sta"][:])
             xc = xcp.tile([P, 2, NT, CW], BF16, name="xc")
             hd[h]["xc"] = xc
             stv = hd[h]["st"][:].rearrange("p t (e f) -> p t e f", f=3)
             dd = statp.tile([P, 2 * NT, 2], F32, name="dd")
-            ptv = statp.tile([P, 2 * NT], F32, name="ptv")
-            hd[h]["ptv"] = ptv
+            ptv = ptt[h % 2]
 
             def some(lo, hi):
                 for c in range(lo, hi):
                     nc.vector.tensor_scalar(
                         out=xc[:, c // NT, c % NT, :],
                         in0=raw[:, c // NT, c % NT, :],
-                        scalar1=negm[:, c : c + 1],
+                        scalar1=negm[:, col(h, c) : col(h, c) + 1],
                         scalar2=None,
                         op0=ALU.add,
                     )
@@ -170,30 +172,25 @@ def tile_entropygraph_pa_t_kernel(tc, q_t, k_t, out):
             nb = NBL[h]
             raw = hd[h]["raw"]
             negm = hd[h]["negm"]
-            pts = statp.tile([P, NT], F32, name="pts")
-            hd[h]["pts"] = pts
             for b in range(nb):
-                c = 2 * NT - nb + b
+                c = SC0 + b
                 nc.scalar.activation(
                     out=junk[:],
                     in_=raw[:, 1, NT - nb + b, :],
                     func=ACT.Square,
                     bias=negm[:, c : c + 1],
                     scale=1.0,
-                    accum_out=pts[:, b : b + 1],
+                    accum_out=ptt[h % 2][:, c : c + 1],
                 )
 
         def tot(h):
-            nat = 2 * NT - NBL[h]
-            stt = stp.tile([P, 2 * NT], F32, name="sta")
+            stt = stp.tile([P, SW], F32, name="sta")
             hd[h]["stt"] = stt
-            nc.tensor.matmul(out=stt[:, 0:nat], lhsT=brepv, rhs=hd[h]["ptv"][:, 0:nat], start=True, stop=True)
-            if NBL[h]:
-                nc.tensor.matmul(out=stt[:, nat : 2 * NT], lhsT=brepv, rhs=hd[h]["pts"][:, 0 : NBL[h]], start=True, stop=True)
+            nc.tensor.matmul(out=stt[:], lhsT=brepv, rhs=ptt[h % 2][:], start=True, stop=True)
 
         def sel(h):
-            tmp = statp.tile([P, 8, 4], F32, name="tmp")
-            var = statp.tile([P, 8], F32, name="var")
+            tmp = statp.tile([P, SW // 4, 4], F32, name="tmp")
+            var = statp.tile([P, SW // 4], F32, name="var")
             kap = statp.tile([P, 4], F32, name="kap")
             sc = statp.tile([P, 4], F32, name="sc")
             bl = statp.tile([P, 2, 4], F32, name="bl")
@@ -203,7 +200,7 @@ def tile_entropygraph_pa_t_kernel(tc, q_t, k_t, out):
             nc.vector.tensor_tensor(
                 out=tmp[:],
                 in0=hd[h]["stt"][:].rearrange("p (b a) -> p b a", a=4),
-                in1=quad[:].unsqueeze(1).to_broadcast([P, 8, 4]),
+                in1=quad[:].unsqueeze(1).to_broadcast([P, SW // 4, 4]),
                 op=ALU.mult,
             )
             return [
@@ -218,13 +215,8 @@ def tile_entropygraph_pa_t_kernel(tc, q_t, k_t, out):
             stb = stp.tile([P, NS], F32, name="stb")
             hd[h]["stb"] = stb
             for nt in range(4):
-                nc.tensor.matmul(
-                    out=stb[:, P * nt : P * (nt + 1)],
-                    lhsT=hd[h]["var"][:, 4 + nt : 5 + nt].to_broadcast([P, P]),
-                    rhs=ident_f[:],
-                    start=True,
-                    stop=True,
-                )
+                g = col(h, NT + 4 * nt) // 4
+                nc.tensor.transpose(stb[:, P * nt : P * (nt + 1)], hd[h]["var"][:, g : g + 1].to_broadcast([P, P]), ident_f[:])
 
         def rsq(h):
             s = sp.tile([P, 4, NS], F32, name="s")
@@ -245,7 +237,7 @@ def tile_entropygraph_pa_t_kernel(tc, q_t, k_t, out):
             for g in range(2):
                 for o in range(2):
                     for b in range(2):
-                        tp = tpp.tile([P, 1024], BF16, name="tp")
+                        tp = bank.tile([P, 1024], BF16, name="tp", tag="bank")
                         for u in range(8):
                             nc.tensor.transpose(tp[:, P * u : P * (u + 1)], xc[:, o, 8 * b + u, P * g : P * (g + 1)], ident_b[:])
                         nc.scalar.copy(out=grp[:, g, o, 1024 * b : 1024 * (b + 1)], in_=tp[:])
@@ -266,7 +258,7 @@ def tile_entropygraph_pa_t_kernel(tc, q_t, k_t, out):
         def mx(h):
             codes = hd[h]["codes"]
             scl = hd[h]["scl"]
-            accs = [accp.tile([P, NS], F32, name="acc") for mt in range(4)]
+            accs = [bank.tile([P, NS], F32, name="acc", tag="bank") for mt in range(4)]
             hd[h]["acc"] = accs
             for g in range(2):
                 for mt in range(4):
@@ -339,9 +331,11 @@ def tile_entropygraph_pa_t_kernel(tc, q_t, k_t, out):
                     w7(i - 1)
                 halves(H)
                 if ok(i + 1):
-                    bsq(i + 1)
                     tco(i + 1)
+                    bsq(i + 1)
                     tot(i + 1)
+                if i % 2 == 0:
+                    logs(i)
                 if ok(i):
                     rsq(i)
                 logs(i)

@@ -23,7 +23,7 @@ NT = 16
 EPS = 1e-6
 SC0 = 32
 SW = 40
-NBL = [4, 4, 4, 4, 4, 4, 4, 4]
+NBL = [8, 8, 8, 8, 8, 8, 8, 8]
 W7_ON = "GGGGGGGG"
 W9_ON = "GGGGGGGG"
 TBUFS = 3

@@ -21,12 +21,7 @@ CH = 4
 CW = 256
 NT = 16
 EPS = 1e-6
-SC0 = 32
-SW = 40
-NBL = [8, 8, 8, 8, 8, 8, 8, 8]
-W7_ON = "GGGGGGGG"
-W9_ON = "GGGGGGGG"
-TBUFS = 3
+TAIL = "A"
 FLOPS = 2 * H * NS * NS * T
 
 
@@ -40,7 +35,7 @@ def tile_entropygraph_pa_t_kernel(tc, q_t, k_t, out):
         cdp = ctx.enter_context(tc.tile_pool(name="cdp", bufs=2))
         statp = ctx.enter_context(tc.tile_pool(name="statp", bufs=2))
         sp = ctx.enter_context(tc.tile_pool(name="sp", bufs=2))
-        tpl = ctx.enter_context(tc.tile_pool(name="tpl", bufs=TBUFS))
+        tpl = ctx.enter_context(tc.tile_pool(name="tpl", bufs=4))
         bank = ctx.enter_context(tc.psum_pool(name="bank", bufs=6))
         stp = ctx.enter_context(tc.psum_pool(name="stp", bufs=1))
 
@@ -67,23 +62,14 @@ def tile_entropygraph_pa_t_kernel(tc, q_t, k_t, out):
         cst = const.tile([P, 2, 4], F32, name="cst")
         nc.vector.tensor_scalar(out=cst[:, 0, :], in0=one[:].to_broadcast([P, 4]), scalar1=EPS, scalar2=None, op0=ALU.mult)
         nc.vector.tensor_scalar(out=cst[:, 1, :], in0=one[:].to_broadcast([P, 4]), scalar1=-1.0 / (T * T), scalar2=None, op0=ALU.mult)
-        junk = const.tile([P, CW], BF16, name="junk")
         bnegv = bneg[:].rearrange("p i j -> p (i j)")
         brepv = brep[:].rearrange("p a i -> p (a i)")
 
-        smt = [const.tile([P, SW], F32, name="smt%d" % n) for n in range(2)]
-        ptt = [const.tile([P, SW], F32, name="ptt%d" % n) for n in range(2)]
-        for n in range(2):
-            nc.vector.memset(smt[n][:], 0.0)
-            nc.vector.memset(ptt[n][:], 0.0)
-
         hd = [dict() for h in range(H)]
 
-        def col(h, c):
-            return c if c < 2 * NT - NBL[h] else SC0 + c - (2 * NT - NBL[h])
-
-        def ok(h):
-            return 0 <= h < H
+        def run(ops):
+            for op in ops:
+                op()
 
         def load(h):
             raw = rawp.tile([P, 2, NT, CW], BF16, name="raw")
@@ -99,108 +85,71 @@ def tile_entropygraph_pa_t_kernel(tc, q_t, k_t, out):
                             in_=src[0, h, SER * a0 : SER * a1, lo : lo + CW].rearrange("(a i) k -> i a k", i=SER),
                         )
 
-        def bsum(h, b):
-            nb = NBL[h]
-            nc.scalar.activation(
-                out=junk[:],
-                in_=hd[h]["raw"][:, 1, NT - nb + b, :],
-                func=ACT.Copy,
-                scale=1.0 / 128.0,
-                accum_out=smt[h % 2][:, SC0 + b : SC0 + b + 1],
-            )
-
-        def bn(h):
-            nat = 2 * NT - NBL[h]
+        def stats(h):
             raw = hd[h]["raw"]
             st = statp.tile([P, 2 * NT, 6], F32, name="st")
             hd[h]["st"] = st
-            for c in range(nat):
+            for c in range(2 * NT):
                 nc.vector.bn_stats(out=st[:, c, :], in_=raw[:, c // NT, c % NT, :])
-            stv = st[:].rearrange("p t (e f) -> p t e f", f=3)
-            nc.vector.tensor_reduce(out=smt[h % 2][:, 0:nat], in_=stv[:, 0:nat, :, 1], axis=AX.X, op=ALU.add)
-
-        def ms(h):
-            sta = stp.tile([P, SW], F32, name="sta")
+            sm = statp.tile([P, 2 * NT], F32, name="sm")
+            nc.vector.tensor_reduce(out=sm[:], in_=st[:].rearrange("p t (e f) -> p t e f", f=3)[:, :, :, 1], axis=AX.X, op=ALU.add)
+            sta = stp.tile([P, 2 * NT], F32, name="sta")
             hd[h]["sta"] = sta
-            nc.tensor.matmul(out=sta[:], lhsT=bnegv, rhs=smt[h % 2][:], start=True, stop=True)
+            nc.tensor.matmul(out=sta[:], lhsT=bnegv, rhs=sm[:], start=True, stop=True)
 
         def centre(h, extra):
-            nat = 2 * NT - NBL[h]
             raw = hd[h]["raw"]
-            negm = statp.tile([P, SW], F32, name="negm")
-            hd[h]["negm"] = negm
+            negm = statp.tile([P, 2 * NT], F32, name="negm")
             nc.vector.tensor_copy(out=negm[:], in_=hd[h]["sta"][:])
             xc = xcp.tile([P, 2, NT, CW], BF16, name="xc")
             hd[h]["xc"] = xc
             stv = hd[h]["st"][:].rearrange("p t (e f) -> p t e f", f=3)
             dd = statp.tile([P, 2 * NT, 2], F32, name="dd")
-            ptv = ptt[h % 2]
-
-            def some(lo, hi):
-                for c in range(lo, hi):
-                    nc.vector.tensor_scalar(
-                        out=xc[:, c // NT, c % NT, :],
-                        in0=raw[:, c // NT, c % NT, :],
-                        scalar1=negm[:, col(h, c) : col(h, c) + 1],
-                        scalar2=None,
-                        op0=ALU.add,
-                    )
-
+            pt = statp.tile([P, 2 * NT], F32, name="pt")
+            hd[h]["pt"] = pt
             small = [
                 lambda: nc.vector.tensor_tensor(
-                    out=dd[:, 0:nat, :],
-                    in0=stv[:, 0:nat, :, 1],
-                    in1=negm[:, 0:nat].unsqueeze(2).to_broadcast([P, nat, 2]),
-                    op=ALU.add,
+                    out=dd[:], in0=stv[:, :, :, 1], in1=negm[:].unsqueeze(2).to_broadcast([P, 2 * NT, 2]), op=ALU.add
                 ),
-                lambda: nc.vector.tensor_tensor(out=dd[:, 0:nat, :], in0=dd[:, 0:nat, :], in1=dd[:, 0:nat, :], op=ALU.mult),
+                lambda: nc.vector.tensor_tensor(out=dd[:], in0=dd[:], in1=dd[:], op=ALU.mult),
                 lambda: nc.vector.scalar_tensor_tensor(
-                    out=dd[:, 0:nat, :], in0=dd[:, 0:nat, :], scalar=128.0, in1=stv[:, 0:nat, :, 2], op0=ALU.mult, op1=ALU.add
+                    out=dd[:], in0=dd[:], scalar=128.0, in1=stv[:, :, :, 2], op0=ALU.mult, op1=ALU.add
                 ),
-                lambda: nc.vector.tensor_reduce(out=ptv[:, 0:nat], in_=dd[:, 0:nat, :], axis=AX.X, op=ALU.add),
+                lambda: nc.vector.tensor_reduce(out=pt[:], in_=dd[:], axis=AX.X, op=ALU.add),
             ]
             both = []
             for n in range(max(len(small), len(extra))):
                 both.extend(extra[n : n + 1])
                 both.extend(small[n : n + 1])
             for n in range(NT):
-                some(2 * n, 2 * n + 2)
-                if n < len(both):
-                    both[n]()
-
-        def bsq(h):
-            nb = NBL[h]
-            raw = hd[h]["raw"]
-            negm = hd[h]["negm"]
-            for b in range(nb):
-                c = SC0 + b
-                nc.scalar.activation(
-                    out=junk[:],
-                    in_=raw[:, 1, NT - nb + b, :],
-                    func=ACT.Square,
-                    bias=negm[:, c : c + 1],
-                    scale=1.0,
-                    accum_out=ptt[h % 2][:, c : c + 1],
-                )
+                for c in (2 * n, 2 * n + 1):
+                    nc.vector.tensor_scalar(
+                        out=xc[:, c // NT, c % NT, :],
+                        in0=raw[:, c // NT, c % NT, :],
+                        scalar1=negm[:, c : c + 1],
+                        scalar2=None,
+                        op0=ALU.add,
+                    )
+                run(both[n : n + 1])
 
         def tot(h):
-            stt = stp.tile([P, SW], F32, name="sta")
+            stt = stp.tile([P, 2 * NT], F32, name="sta")
             hd[h]["stt"] = stt
-            nc.tensor.matmul(out=stt[:], lhsT=brepv, rhs=ptt[h % 2][:], start=True, stop=True)
+            nc.tensor.matmul(out=stt[:], lhsT=brepv, rhs=hd[h]["pt"][:], start=True, stop=True)
 
         def sel(h):
-            tmp = statp.tile([P, SW // 4, 4], F32, name="tmp")
-            var = statp.tile([P, SW // 4], F32, name="var")
+            tmp = statp.tile([P, 8, 4], F32, name="tmp")
+            var = statp.tile([P, 8], F32, name="var")
             kap = statp.tile([P, 4], F32, name="kap")
             sc = statp.tile([P, 4], F32, name="sc")
-            bl = statp.tile([P, 2, 4], F32, name="bl")
+            bl = statp.tile([P, 2, 4], F32, name="bl", bufs=4)
             hd[h]["var"] = var
             hd[h]["sc"] = sc
             hd[h]["bl"] = bl
             nc.vector.tensor_tensor(
                 out=tmp[:],
                 in0=hd[h]["stt"][:].rearrange("p (b a) -> p b a", a=4),
-                in1=quad[:].unsqueeze(1).to_broadcast([P, SW // 4, 4]),
+                in1=quad[:].unsqueeze(1).to_broadcast([P, 8, 4]),
                 op=ALU.mult,
             )
             return [
@@ -215,8 +164,7 @@ def tile_entropygraph_pa_t_kernel(tc, q_t, k_t, out):
             stb = stp.tile([P, NS], F32, name="stb")
             hd[h]["stb"] = stb
             for nt in range(4):
-                g = col(h, NT + 4 * nt) // 4
-                nc.tensor.transpose(stb[:, P * nt : P * (nt + 1)], hd[h]["var"][:, g : g + 1].to_broadcast([P, P]), ident_f[:])
+                nc.tensor.transpose(stb[:, P * nt : P * (nt + 1)], hd[h]["var"][:, 4 + nt : 5 + nt].to_broadcast([P, P]), ident_f[:])
 
         def rsq(h):
             s = sp.tile([P, 4, NS], F32, name="s")
@@ -230,7 +178,7 @@ def tile_entropygraph_pa_t_kernel(tc, q_t, k_t, out):
                     scale=hd[h]["sc"][:, mt : mt + 1],
                 )
 
-        def tco(h):
+        def tco(h, share):
             xc = hd[h]["xc"]
             grp = grpp.tile([P, 2, 2, 2048], BF16, name="grp", align_bytes=64)
             hd[h]["grp"] = grp
@@ -240,24 +188,18 @@ def tile_entropygraph_pa_t_kernel(tc, q_t, k_t, out):
                         tp = bank.tile([P, 1024], BF16, name="tp", tag="bank")
                         for u in range(8):
                             nc.tensor.transpose(tp[:, P * u : P * (u + 1)], xc[:, o, 8 * b + u, P * g : P * (g + 1)], ident_b[:])
-                        nc.scalar.copy(out=grp[:, g, o, 1024 * b : 1024 * (b + 1)], in_=tp[:])
-                        n = 4 * g + 2 * o + b
-                        if ok(h + 1) and n < NBL[h + 1]:
-                            bsum(h + 1, n)
+                        if share and b == 1:
+                            nc.vector.tensor_copy(out=grp[:, g, o, 1024 * b : 1024 * (b + 1)], in_=tp[:])
+                        else:
+                            nc.scalar.copy(out=grp[:, g, o, 1024 * b : 1024 * (b + 1)], in_=tp[:])
 
         def quant(h):
             grp = hd[h]["grp"]
             codes = cdp.tile([P, 2, 2, NS], U32, name="codes", align_bytes=64)
             scl = cdp.tile([P, 2, 2, NS], U8, name="scl", align_bytes=64)
-            hd[h]["codes"] = codes
-            hd[h]["scl"] = scl
             for g in range(2):
                 for o in range(2):
                     nc.vector.quantize_mx(out=codes[:, g, o, :].bitcast(FP8X4), scales=scl[:, g, o, :], in_=grp[:, g, o, :])
-
-        def mx(h):
-            codes = hd[h]["codes"]
-            scl = hd[h]["scl"]
             accs = [bank.tile([P, NS], F32, name="acc", tag="bank") for mt in range(4)]
             hd[h]["acc"] = accs
             for g in range(2):
@@ -272,34 +214,26 @@ def tile_entropygraph_pa_t_kernel(tc, q_t, k_t, out):
                         stop=(g == 1),
                     )
 
-        def w6(h):
+        def corr(h, square_on):
             t = tpl.tile([P, 4, NS], F32, name="t")
             hd[h]["t"] = t
             for mt in range(4):
                 nc.vector.tensor_tensor(out=t[:, mt, :], in0=hd[h]["acc"][mt][:], in1=hd[h]["s"][:, mt, :], op=ALU.mult)
-
-        def w7(h):
-            t = hd[h]["t"]
             for mt in range(4):
-                if W7_ON[h] == "G":
-                    nc.gpsimd.tensor_tensor(out=t[:, mt, :], in0=t[:, mt, :], in1=t[:, mt, :], op=ALU.mult)
-                else:
-                    nc.scalar.activation(out=t[:, mt, :], in_=t[:, mt, :], func=ACT.Square)
+                square_on.tensor_tensor(out=t[:, mt, :], in0=t[:, mt, :], in1=t[:, mt, :], op=ALU.mult)
 
         def ln(h):
             t = hd[h]["t"]
             for mt in range(4):
                 nc.scalar.activation(out=t[:, mt, :], in_=t[:, mt, :], func=ACT.Ln, bias=c1[:], scale=hd[h]["bl"][:, 1, mt : mt + 1])
 
-        def w9(h):
+        def finish(h, on_vector):
             t = hd[h]["t"]
             ov = out[0, h, :, :].rearrange("(mt m) j -> m mt j", m=P)
             for half in range(2):
                 sl = t[:, 2 * half : 2 * half + 2, :]
-                if W9_ON[h] == "V":
+                if on_vector:
                     nc.vector.tensor_scalar(out=sl, in0=sl, scalar1=-0.5, scalar2=None, op0=ALU.mult)
-                elif W9_ON[h] == "S":
-                    nc.scalar.activation(out=sl, in_=sl, func=ACT.Copy, scale=-0.5)
                 else:
                     nc.gpsimd.tensor_scalar(out=sl, in0=sl, scalar1=-0.5, scalar2=0.0, op0=ALU.mult, op1=ALU.add)
                 nc.sync.dma_start(out=ov[:, 2 * half : 2 * half + 2, :], in_=sl)
@@ -307,51 +241,49 @@ def tile_entropygraph_pa_t_kernel(tc, q_t, k_t, out):
         with tc.manual_schedule():
             for h in range(3):
                 load(h)
-            done = {"ln": 0, "w9": 0}
-
-            def logs(upto):
-                while done["ln"] < min(upto, H):
-                    ln(done["ln"])
-                    done["ln"] += 1
-
-            def halves(most):
-                n = 0
-                while done["w9"] < done["ln"] and n < most:
-                    w9(done["w9"])
-                    done["w9"] += 1
-                    n += 1
-
-            for b in range(NBL[0]):
-                bsum(0, b)
-            for i in range(-2, H + 1):
-                if i >= -1 and ok(i + 4):
+            for i in range(-2, H - 2):
+                if i >= -1 and i + 4 < H:
                     load(i + 4)
-                if ok(i - 1):
-                    w6(i - 1)
-                    w7(i - 1)
-                halves(H)
-                if ok(i + 1):
-                    tco(i + 1)
-                    bsq(i + 1)
+                if i >= 1:
+                    corr(i - 1, nc.gpsimd)
+                if i >= 2:
+                    finish(i - 2, False)
+                if i >= -1:
+                    tco(i + 1, False)
                     tot(i + 1)
-                if i % 2 == 0:
-                    logs(i)
-                if ok(i):
+                if i >= 1 and i % 2 == 0:
+                    ln(i - 1)
+                if i >= 0:
                     rsq(i)
-                logs(i)
-                if ok(i + 2):
-                    bn(i + 2)
-                extra = sel(i + 1) if ok(i + 1) else []
-                if ok(i + 2):
-                    ms(i + 2)
-                if ok(i):
+                if i >= 1 and i % 2 == 1:
+                    ln(i - 1)
+                stats(i + 2)
+                extra = sel(i + 1) if i >= -1 else []
+                if i >= 0:
                     quant(i)
-                    mx(i)
-                if ok(i + 2):
-                    centre(i + 2, extra)
-                else:
-                    for op in extra:
-                        op()
-                if ok(i + 1):
+                centre(i + 2, extra)
+                if i >= -1:
                     bcast(i + 1)
-            halves(H)
+            corr(H - 3, nc.gpsimd)
+            finish(H - 4, False)
+            tco(H - 1, True)
+            tot(H - 1)
+            if TAIL == "A":
+                ln(H - 3)
+            quant(H - 2)
+            run(sel(H - 1))
+            bcast(H - 1)
+            rsq(H - 2)
+            rsq(H - 1)
+            quant(H - 1)
+            if TAIL == "A":
+                finish(H - 3, False)
+            corr(H - 2, nc.gpsimd)
+            corr(H - 1, nc.vector)
+            if TAIL == "B":
+                ln(H - 3)
+                finish(H - 3, False)
+            ln(H - 2)
+            finish(H - 2, True)
+            ln(H - 1)
+            finish(H - 1, True)

@@ -16,12 +16,14 @@ H = 8
 NS = 512
 T = 1024
 P = 128
-SER = 32
-CH = 4
-CW = 256
-NT = 16
+SER = 64
+CH = 2
+CW = 512
+NT = 8
+MTT = P // SER
 EPS = 1e-6
 TAIL = "A"
+SG = 0
 FLOPS = 2 * H * NS * NS * T
 
 
@@ -45,15 +47,15 @@ def tile_entropygraph_pa_t_kernel(tc, q_t, k_t, out):
         nc.vector.tensor_copy(out=ident_b[:], in_=ident_f[:])
         mask = const.tile([P, SER], F32, name="mask")
         nc.vector.tensor_reduce(out=mask[:], in_=ident_f[:].rearrange("p (i j) -> p i j", j=CH), axis=AX.X, op=ALU.add)
-        quad = const.tile([P, 4], F32, name="quad")
+        quad = const.tile([P, MTT], F32, name="quad")
         nc.vector.tensor_reduce(out=quad[:], in_=ident_f[:].rearrange("p (a i) -> p a i", i=SER), axis=AX.X, op=ALU.add)
         bneg = const.tile([P, SER, CH], F32, name="bneg")
         nc.vector.tensor_scalar(
-            out=bneg[:], in0=mask[:].unsqueeze(2).to_broadcast([P, SER, CH]), scalar1=-0.125, scalar2=None, op0=ALU.mult
+            out=bneg[:], in0=mask[:].unsqueeze(2).to_broadcast([P, SER, CH]), scalar1=-0.5 / CH, scalar2=None, op0=ALU.mult
         )
-        brep = const.tile([P, 4, SER], F32, name="brep")
+        brep = const.tile([P, MTT, SER], F32, name="brep")
         nc.vector.tensor_scalar(
-            out=brep[:], in0=mask[:].unsqueeze(1).to_broadcast([P, 4, SER]), scalar1=1.0 / T, scalar2=None, op0=ALU.mult
+            out=brep[:], in0=mask[:].unsqueeze(1).to_broadcast([P, MTT, SER]), scalar1=1.0 / T, scalar2=None, op0=ALU.mult
         )
         one = const.tile([P, 1], F32, name="one")
         nc.vector.memset(one[:], 1.0)
@@ -74,7 +76,7 @@ def tile_entropygraph_pa_t_kernel(tc, q_t, k_t, out):
         def load(h):
             raw = rawp.tile([P, 2, NT, CW], BF16, name="raw")
             hd[h]["raw"] = raw
-            cuts = ((0, 4), (4, NT)) if h == 0 else ((0, NT),)
+            cuts = ((0, 2), (2, NT)) if h == 0 else ((0, NT),)
             for o in range(2):
                 src = (q_t, k_t)[o]
                 for a0, a1 in cuts:
@@ -113,7 +115,7 @@ def tile_entropygraph_pa_t_kernel(tc, q_t, k_t, out):
                 ),
                 lambda: nc.vector.tensor_tensor(out=dd[:], in0=dd[:], in1=dd[:], op=ALU.mult),
                 lambda: nc.vector.scalar_tensor_tensor(
-                    out=dd[:], in0=dd[:], scalar=128.0, in1=stv[:, :, :, 2], op0=ALU.mult, op1=ALU.add
+                    out=dd[:], in0=dd[:], scalar=CW / 2.0, in1=stv[:, :, :, 2], op0=ALU.mult, op1=ALU.add
                 ),
                 lambda: nc.vector.tensor_reduce(out=pt[:], in_=dd[:], axis=AX.X, op=ALU.add),
             ]
@@ -121,8 +123,8 @@ def tile_entropygraph_pa_t_kernel(tc, q_t, k_t, out):
             for n in range(max(len(small), len(extra))):
                 both.extend(extra[n : n + 1])
                 both.extend(small[n : n + 1])
-            for n in range(NT):
-                for c in (2 * n, 2 * n + 1):
+            for n in range(2 * NT):
+                for c in (n,):
                     nc.vector.tensor_scalar(
                         out=xc[:, c // NT, c % NT, :],
                         in0=raw[:, c // NT, c % NT, :],
@@ -138,7 +140,7 @@ def tile_entropygraph_pa_t_kernel(tc, q_t, k_t, out):
             nc.tensor.matmul(out=stt[:], lhsT=brepv, rhs=hd[h]["pt"][:], start=True, stop=True)
 
         def sel(h):
-            tmp = statp.tile([P, 8, 4], F32, name="tmp")
+            tmp = statp.tile([P, 8, MTT], F32, name="tmp")
             var = statp.tile([P, 8], F32, name="var")
             kap = statp.tile([P, 4], F32, name="kap")
             sc = statp.tile([P, 4], F32, name="sc")
@@ -148,8 +150,8 @@ def tile_entropygraph_pa_t_kernel(tc, q_t, k_t, out):
             hd[h]["bl"] = bl
             nc.vector.tensor_tensor(
                 out=tmp[:],
-                in0=hd[h]["stt"][:].rearrange("p (b a) -> p b a", a=4),
-                in1=quad[:].unsqueeze(1).to_broadcast([P, 8, 4]),
+                in0=hd[h]["stt"][:].rearrange("p (b a) -> p b a", a=MTT),
+                in1=quad[:].unsqueeze(1).to_broadcast([P, 8, MTT]),
                 op=ALU.mult,
             )
             return [
@@ -185,13 +187,17 @@ def tile_entropygraph_pa_t_kernel(tc, q_t, k_t, out):
             for g in range(2):
                 for o in range(2):
                     for b in range(2):
-                        tp = bank.tile([P, 1024], BF16, name="tp", tag="bank")
-                        for u in range(8):
-                            nc.tensor.transpose(tp[:, P * u : P * (u + 1)], xc[:, o, 8 * b + u, P * g : P * (g + 1)], ident_b[:])
+                        tp = bank.tile([P, 2, 4, P], BF16, name="tp", tag="bank")
+                        for u in range(2):
+                            for a in range(4):
+                                lo = P * (2 * g + u)
+                                nc.tensor.transpose(tp[:, u, a, :], xc[:, o, 4 * b + a, lo : lo + P], ident_b[:])
+                        dst = grp[:, g, o, 1024 * b : 1024 * (b + 1)].rearrange("p (m u j) -> p m u j", u=2, j=CH)
+                        src = tp[:].rearrange("p u a (i j) -> p (a i) u j", j=CH)
                         if share and b == 1:
-                            nc.vector.tensor_copy(out=grp[:, g, o, 1024 * b : 1024 * (b + 1)], in_=tp[:])
+                            nc.vector.tensor_copy(out=dst, in_=src)
                         else:
-                            nc.scalar.copy(out=grp[:, g, o, 1024 * b : 1024 * (b + 1)], in_=tp[:])
+                            nc.scalar.copy(out=dst, in_=src)
 
         def quant(h):
             grp = hd[h]["grp"]
@@ -214,13 +220,21 @@ def tile_entropygraph_pa_t_kernel(tc, q_t, k_t, out):
                         stop=(g == 1),
                     )
 
-        def corr(h, square_on):
+        def corr(h, square_on, sg):
             t = tpl.tile([P, 4, NS], F32, name="t")
             hd[h]["t"] = t
+            s = hd[h]["s"]
             for mt in range(4):
-                nc.vector.tensor_tensor(out=t[:, mt, :], in0=hd[h]["acc"][mt][:], in1=hd[h]["s"][:, mt, :], op=ALU.mult)
+                if mt >= 4 - sg:
+                    nc.scalar.activation(out=t[:, mt, :], in_=hd[h]["acc"][mt][:], func=ACT.Square)
+                else:
+                    nc.vector.tensor_tensor(out=t[:, mt, :], in0=hd[h]["acc"][mt][:], in1=s[:, mt, :], op=ALU.mult)
             for mt in range(4):
-                square_on.tensor_tensor(out=t[:, mt, :], in0=t[:, mt, :], in1=t[:, mt, :], op=ALU.mult)
+                if mt >= 4 - sg:
+                    square_on.tensor_tensor(out=t[:, mt, :], in0=t[:, mt, :], in1=s[:, mt, :], op=ALU.mult)
+                    square_on.tensor_tensor(out=t[:, mt, :], in0=t[:, mt, :], in1=s[:, mt, :], op=ALU.mult)
+                else:
+                    square_on.tensor_tensor(out=t[:, mt, :], in0=t[:, mt, :], in1=t[:, mt, :], op=ALU.mult)
 
         def ln(h):
             t = hd[h]["t"]
@@ -245,7 +259,7 @@ def tile_entropygraph_pa_t_kernel(tc, q_t, k_t, out):
                 if i >= -1 and i + 4 < H:
                     load(i + 4)
                 if i >= 1:
-                    corr(i - 1, nc.gpsimd)
+                    corr(i - 1, nc.gpsimd, SG)
                 if i >= 2:
                     finish(i - 2, False)
                 if i >= -1:
@@ -264,7 +278,7 @@ def tile_entropygraph_pa_t_kernel(tc, q_t, k_t, out):
                 centre(i + 2, extra)
                 if i >= -1:
                     bcast(i + 1)
-            corr(H - 3, nc.gpsimd)
+            corr(H - 3, nc.gpsimd, SG)
             finish(H - 4, False)
             tco(H - 1, True)
             tot(H - 1)
@@ -278,8 +292,8 @@ def tile_entropygraph_pa_t_kernel(tc, q_t, k_t, out):
             quant(H - 1)
             if TAIL == "A":
                 finish(H - 3, False)
-            corr(H - 2, nc.gpsimd)
-            corr(H - 1, nc.vector)
+            corr(H - 2, nc.gpsimd, 0)
+            corr(H - 1, nc.vector, 0)
             if TAIL == "B":
                 ln(H - 3)
                 finish(H - 3, False)

@@ -23,7 +23,10 @@ NT = 8
 MTT = P // SER
 EPS = 1e-6
 TAIL = "A"
-SG = 0
+SG = 2
+SGT = 0
+SGT7 = 0
+F6V = 1
 FLOPS = 2 * H * NS * NS * T
 
 
@@ -278,7 +281,7 @@ def tile_entropygraph_pa_t_kernel(tc, q_t, k_t, out):
                 centre(i + 2, extra)
                 if i >= -1:
                     bcast(i + 1)
-            corr(H - 3, nc.gpsimd, SG)
+            corr(H - 3, nc.gpsimd, SGT)
             finish(H - 4, False)
             tco(H - 1, True)
             tot(H - 1)
@@ -286,18 +289,24 @@ def tile_entropygraph_pa_t_kernel(tc, q_t, k_t, out):
                 ln(H - 3)
             quant(H - 2)
             run(sel(H - 1))
-            bcast(H - 1)
-            rsq(H - 2)
-            rsq(H - 1)
-            quant(H - 1)
+            if TAIL == "D":
+                rsq(H - 2)
+                quant(H - 1)
+                bcast(H - 1)
+                rsq(H - 1)
+            else:
+                bcast(H - 1)
+                rsq(H - 2)
+                rsq(H - 1)
+                quant(H - 1)
             if TAIL == "A":
                 finish(H - 3, False)
-            corr(H - 2, nc.gpsimd, 0)
-            corr(H - 1, nc.vector, 0)
-            if TAIL == "B":
+            corr(H - 2, nc.gpsimd, SGT)
+            corr(H - 1, nc.vector, SGT7)
+            if TAIL != "A":
                 ln(H - 3)
                 finish(H - 3, False)
             ln(H - 2)
-            finish(H - 2, True)
+            finish(H - 2, F6V == 1)
             ln(H - 1)
             finish(H - 1, True)

@@ -23,7 +23,7 @@ NT = 8
 MTT = P // SER
 EPS = 1e-6
 TAIL = "A"
-SG = 2
+SG = 1
 SGT = 0
 SGT7 = 0
 F6V = 1

@@ -16,11 +16,8 @@ H = 8
 NS = 512
 T = 1024
 P = 128
-SER = 64
-CH = 2
-CW = 512
-NT = 8
-MTT = P // SER
+NT = 4
+HALF = 512
 EPS = 1e-6
 TAIL = "A"
 SG = 1
@@ -41,34 +38,18 @@ def tile_entropygraph_pa_t_kernel(tc, q_t, k_t, out):
         statp = ctx.enter_context(tc.tile_pool(name="statp", bufs=2))
         sp = ctx.enter_context(tc.tile_pool(name="sp", bufs=2))
         tpl = ctx.enter_context(tc.tile_pool(name="tpl", bufs=4))
-        bank = ctx.enter_context(tc.psum_pool(name="bank", bufs=6))
+        bank = ctx.enter_context(tc.psum_pool(name="bank", bufs=7))
         stp = ctx.enter_context(tc.psum_pool(name="stp", bufs=1))
 
         ident_f = const.tile([P, P], F32, name="ident_f")
         make_identity(nc, ident_f[:])
-        ident_b = const.tile([P, P], BF16, name="ident_b")
-        nc.vector.tensor_copy(out=ident_b[:], in_=ident_f[:])
-        mask = const.tile([P, SER], F32, name="mask")
-        nc.vector.tensor_reduce(out=mask[:], in_=ident_f[:].rearrange("p (i j) -> p i j", j=CH), axis=AX.X, op=ALU.add)
-        quad = const.tile([P, MTT], F32, name="quad")
-        nc.vector.tensor_reduce(out=quad[:], in_=ident_f[:].rearrange("p (a i) -> p a i", i=SER), axis=AX.X, op=ALU.add)
-        bneg = const.tile([P, SER, CH], F32, name="bneg")
-        nc.vector.tensor_scalar(
-            out=bneg[:], in0=mask[:].unsqueeze(2).to_broadcast([P, SER, CH]), scalar1=-0.5 / CH, scalar2=None, op0=ALU.mult
-        )
-        brep = const.tile([P, MTT, SER], F32, name="brep")
-        nc.vector.tensor_scalar(
-            out=brep[:], in0=mask[:].unsqueeze(1).to_broadcast([P, MTT, SER]), scalar1=1.0 / T, scalar2=None, op0=ALU.mult
-        )
         one = const.tile([P, 1], F32, name="one")
         nc.vector.memset(one[:], 1.0)
         c1 = const.tile([P, 1], F32, name="c1")
         nc.vector.tensor_scalar(out=c1[:], in0=one[:], scalar1=EPS, scalar2=None, op0=ALU.add)
         cst = const.tile([P, 2, 4], F32, name="cst")
-        nc.vector.tensor_scalar(out=cst[:, 0, :], in0=one[:].to_broadcast([P, 4]), scalar1=EPS, scalar2=None, op0=ALU.mult)
-        nc.vector.tensor_scalar(out=cst[:, 1, :], in0=one[:].to_broadcast([P, 4]), scalar1=-1.0 / (T * T), scalar2=None, op0=ALU.mult)
-        bnegv = bneg[:].rearrange("p i j -> p (i j)")
-        brepv = brep[:].rearrange("p a i -> p (a i)")
+        nc.vector.tensor_scalar(out=cst[:, 0, :], in0=one[:].to_broadcast([P, 4]), scalar1=T * EPS, scalar2=None, op0=ALU.mult)
+        nc.vector.tensor_scalar(out=cst[:, 1, :], in0=one[:].to_broadcast([P, 4]), scalar1=-1.0 / T, scalar2=None, op0=ALU.mult)
 
         hd = [dict() for h in range(H)]
 
@@ -77,48 +58,46 @@ def tile_entropygraph_pa_t_kernel(tc, q_t, k_t, out):
                 op()
 
         def load(h):
-            raw = rawp.tile([P, 2, NT, CW], BF16, name="raw")
+            raw = rawp.tile([P, 2, NT, T], BF16, name="raw")
             hd[h]["raw"] = raw
-            cuts = ((0, 2), (2, NT)) if h == 0 else ((0, NT),)
+            cuts = ((0, 1), (1, 2), (2, NT)) if h == 0 else ((0, NT),)
             for o in range(2):
                 src = (q_t, k_t)[o]
                 for a0, a1 in cuts:
-                    for j in range(CH):
-                        lo = o + j * CW
-                        nc.sync.dma_start(
-                            out=raw[j:P:CH, o, a0:a1, :],
-                            in_=src[0, h, SER * a0 : SER * a1, lo : lo + CW].rearrange("(a i) k -> i a k", i=SER),
-                        )
+                    nc.sync.dma_start(
+                        out=raw[:, o, a0:a1, :],
+                        in_=src[0, h, P * a0 : P * a1, o : o + T].rearrange("(a p) k -> p a k", p=P),
+                    )
 
         def stats(h):
             raw = hd[h]["raw"]
-            st = statp.tile([P, 2 * NT, 6], F32, name="st")
+            st = statp.tile([P, 2 * NT, 2, 6], F32, name="st")
             hd[h]["st"] = st
             for c in range(2 * NT):
-                nc.vector.bn_stats(out=st[:, c, :], in_=raw[:, c // NT, c % NT, :])
-            sm = statp.tile([P, 2 * NT], F32, name="sm")
-            nc.vector.tensor_reduce(out=sm[:], in_=st[:].rearrange("p t (e f) -> p t e f", f=3)[:, :, :, 1], axis=AX.X, op=ALU.add)
-            sta = stp.tile([P, 2 * NT], F32, name="sta")
-            hd[h]["sta"] = sta
-            nc.tensor.matmul(out=sta[:], lhsT=bnegv, rhs=sm[:], start=True, stop=True)
+                for half in range(2):
+                    nc.vector.bn_stats(
+                        out=st[:, c, half, :], in_=raw[:, c // NT, c % NT, HALF * half : HALF * (half + 1)]
+                    )
 
         def centre(h, extra):
             raw = hd[h]["raw"]
+            stv = hd[h]["st"][:].rearrange("p t b (e f) -> p t (b e) f", f=3)
+            sm = statp.tile([P, 2 * NT], F32, name="sm")
+            nc.vector.tensor_reduce(out=sm[:], in_=stv[:, :, :, 1], axis=AX.X, op=ALU.add)
             negm = statp.tile([P, 2 * NT], F32, name="negm")
-            nc.vector.tensor_copy(out=negm[:], in_=hd[h]["sta"][:])
-            xc = xcp.tile([P, 2, NT, CW], BF16, name="xc")
+            nc.vector.tensor_scalar(out=negm[:], in0=sm[:], scalar1=-0.25, scalar2=None, op0=ALU.mult)
+            xc = xcp.tile([P, 2, NT, T], BF16, name="xc")
             hd[h]["xc"] = xc
-            stv = hd[h]["st"][:].rearrange("p t (e f) -> p t e f", f=3)
-            dd = statp.tile([P, 2 * NT, 2], F32, name="dd")
+            dd = statp.tile([P, 2 * NT, 4], F32, name="dd")
             pt = statp.tile([P, 2 * NT], F32, name="pt")
             hd[h]["pt"] = pt
             small = [
                 lambda: nc.vector.tensor_tensor(
-                    out=dd[:], in0=stv[:, :, :, 1], in1=negm[:].unsqueeze(2).to_broadcast([P, 2 * NT, 2]), op=ALU.add
+                    out=dd[:], in0=stv[:, :, :, 1], in1=negm[:].unsqueeze(2).to_broadcast([P, 2 * NT, 4]), op=ALU.add
                 ),
                 lambda: nc.vector.tensor_tensor(out=dd[:], in0=dd[:], in1=dd[:], op=ALU.mult),
                 lambda: nc.vector.scalar_tensor_tensor(
-                    out=dd[:], in0=dd[:], scalar=CW / 2.0, in1=stv[:, :, :, 2], op0=ALU.mult, op1=ALU.add
+                    out=dd[:], in0=dd[:], scalar=T / 4.0, in1=stv[:, :, :, 2], op0=ALU.mult, op1=ALU.add
                 ),
                 lambda: nc.vector.tensor_reduce(out=pt[:], in_=dd[:], axis=AX.X, op=ALU.add),
             ]
@@ -126,42 +105,30 @@ def tile_entropygraph_pa_t_kernel(tc, q_t, k_t, out):
             for n in range(max(len(small), len(extra))):
                 both.extend(extra[n : n + 1])
                 both.extend(small[n : n + 1])
-            for n in range(2 * NT):
-                for c in (n,):
-                    nc.vector.tensor_scalar(
-                        out=xc[:, c // NT, c % NT, :],
-                        in0=raw[:, c // NT, c % NT, :],
-                        scalar1=negm[:, c : c + 1],
-                        scalar2=None,
-                        op0=ALU.add,
-                    )
-                run(both[n : n + 1])
-
-        def tot(h):
-            stt = stp.tile([P, 2 * NT], F32, name="sta")
-            hd[h]["stt"] = stt
-            nc.tensor.matmul(out=stt[:], lhsT=brepv, rhs=hd[h]["pt"][:], start=True, stop=True)
+            for c in range(2 * NT):
+                nc.vector.tensor_scalar(
+                    out=xc[:, c // NT, c % NT, :],
+                    in0=raw[:, c // NT, c % NT, :],
+                    scalar1=negm[:, c : c + 1],
+                    scalar2=None,
+                    op0=ALU.add,
+                )
+                run(both[c : c + 1])
+            run(both[2 * NT :])
 
         def sel(h):
-            tmp = statp.tile([P, 8, MTT], F32, name="tmp")
-            var = statp.tile([P, 8], F32, name="var")
+            pt = hd[h]["pt"]
             kap = statp.tile([P, 4], F32, name="kap")
             sc = statp.tile([P, 4], F32, name="sc")
             bl = statp.tile([P, 2, 4], F32, name="bl", bufs=4)
-            hd[h]["var"] = var
             hd[h]["sc"] = sc
             hd[h]["bl"] = bl
-            nc.vector.tensor_tensor(
-                out=tmp[:],
-                in0=hd[h]["stt"][:].rearrange("p (b a) -> p b a", a=MTT),
-                in1=quad[:].unsqueeze(1).to_broadcast([P, 8, MTT]),
-                op=ALU.mult,
-            )
             return [
-                lambda: nc.vector.tensor_reduce(out=var[:], in_=tmp[:], axis=AX.X, op=ALU.add),
-                lambda: nc.vector.tensor_scalar(out=kap[:], in0=var[:, 0:4], scalar1=EPS, scalar2=None, op0=ALU.max),
+                lambda: nc.vector.tensor_scalar(out=kap[:], in0=pt[:, 0:4], scalar1=T * EPS, scalar2=None, op0=ALU.max),
                 lambda: nc.vector.reciprocal(out=kap[:], in_=kap[:]),
-                lambda: nc.vector.tensor_tensor(out=sc[:], in0=kap[:], in1=var[:, 0:4], op=ALU.mult),
+                lambda: nc.vector.scalar_tensor_tensor(
+                    out=sc[:], in0=pt[:, 0:4], scalar=1.0 / T, in1=kap[:], op0=ALU.mult, op1=ALU.mult
+                ),
                 lambda: nc.vector.tensor_tensor(out=bl[:], in0=kap[:].unsqueeze(1).to_broadcast([P, 2, 4]), in1=cst[:], op=ALU.mult),
             ]
 
@@ -169,7 +136,7 @@ def tile_entropygraph_pa_t_kernel(tc, q_t, k_t, out):
             stb = stp.tile([P, NS], F32, name="stb")
             hd[h]["stb"] = stb
             for nt in range(4):
-                nc.tensor.transpose(stb[:, P * nt : P * (nt + 1)], hd[h]["var"][:, 4 + nt : 5 + nt].to_broadcast([P, P]), ident_f[:])
+                nc.tensor.transpose(stb[:, P * nt : P * (nt + 1)], hd[h]["pt"][:, 4 + nt : 5 + nt].to_broadcast([P, P]), ident_f[:])
 
         def rsq(h):
             s = sp.tile([P, 4, NS], F32, name="s")
@@ -190,13 +157,13 @@ def tile_entropygraph_pa_t_kernel(tc, q_t, k_t, out):
             for g in range(2):
                 for o in range(2):
                     for b in range(2):
-                        tp = bank.tile([P, 2, 4, P], BF16, name="tp", tag="bank")
-                        for u in range(2):
-                            for a in range(4):
-                                lo = P * (2 * g + u)
-                                nc.tensor.transpose(tp[:, u, a, :], xc[:, o, 4 * b + a, lo : lo + P], ident_b[:])
-                        dst = grp[:, g, o, 1024 * b : 1024 * (b + 1)].rearrange("p (m u j) -> p m u j", u=2, j=CH)
-                        src = tp[:].rearrange("p u a (i j) -> p (a i) u j", j=CH)
+                        tp = bank.tile([P, 2, 2, P], F32, name="tp", tag="bank")
+                        for a in range(2):
+                            words = xc[:, o, 2 * b + a, :].bitcast(F32)
+                            for u in range(2):
+                                nc.tensor.transpose(tp[:, u, a, :], words[:, 256 * g + u : 256 * (g + 1) : 2], ident_f[:])
+                        dst = grp[:, g, o, 1024 * b : 1024 * (b + 1)].bitcast(F32).rearrange("p (r u) -> p r u", u=2)
+                        src = tp[:].rearrange("p u a i -> p (a i) u")
                         if share and b == 1:
                             nc.vector.tensor_copy(out=dst, in_=src)
                         else:
@@ -267,7 +234,6 @@ def tile_entropygraph_pa_t_kernel(tc, q_t, k_t, out):
                     finish(i - 2, False)
                 if i >= -1:
                     tco(i + 1, False)
-                    tot(i + 1)
                 if i >= 1 and i % 2 == 0:
                     ln(i - 1)
                 if i >= 0:
@@ -284,7 +250,6 @@ def tile_entropygraph_pa_t_kernel(tc, q_t, k_t, out):
             corr(H - 3, nc.gpsimd, SGT)
             finish(H - 4, False)
             tco(H - 1, True)
-            tot(H - 1)
             if TAIL == "A":
                 ln(H - 3)
             quant(H - 2)

@@ -24,6 +24,7 @@ SG = 1
 SGT = 0
 SGT7 = 0
 F6V = 1
+SKT = (3, 3, 2, 1, 1, 1, 1, 1)
 FLOPS = 2 * H * NS * NS * T
 
 
@@ -37,6 +38,7 @@ def tile_entropygraph_pa_t_kernel(tc, q_t, k_t, out):
         cdp = ctx.enter_context(tc.tile_pool(name="cdp", bufs=2))
         statp = ctx.enter_context(tc.tile_pool(name="statp", bufs=2))
         sp = ctx.enter_context(tc.tile_pool(name="sp", bufs=2))
+        junkp = ctx.enter_context(tc.tile_pool(name="junkp", bufs=2))
         tpl = ctx.enter_context(tc.tile_pool(name="tpl", bufs=4))
         bank = ctx.enter_context(tc.psum_pool(name="bank", bufs=7))
         stp = ctx.enter_context(tc.psum_pool(name="stp", bufs=1))
@@ -71,29 +73,49 @@ def tile_entropygraph_pa_t_kernel(tc, q_t, k_t, out):
 
         def stats(h):
             raw = hd[h]["raw"]
-            st = statp.tile([P, 2 * NT, 2, 6], F32, name="st")
+            nv = 2 * NT - SKT[h]
+            st = statp.tile([P, nv, 2, 6], F32, name="st")
             hd[h]["st"] = st
-            for c in range(2 * NT):
+            for c in range(nv):
                 for half in range(2):
                     nc.vector.bn_stats(
                         out=st[:, c, half, :], in_=raw[:, c // NT, c % NT, HALF * half : HALF * (half + 1)]
                     )
 
+        def statsc(h):
+            raw = hd[h]["raw"]
+            ns = SKT[h]
+            sx = statp.tile([P, ns], F32, name="sx")
+            sneg = statp.tile([P, ns], F32, name="sneg")
+            spt = statp.tile([P, ns], F32, name="spt")
+            hd[h]["sneg"] = sneg
+            hd[h]["spt"] = spt
+            for c in range(ns):
+                junk = junkp.tile([P, T], BF16, name="junk")
+                nc.scalar.activation(out=junk[:], in_=raw[:, 1, NT - ns + c, :], func=ACT.Copy, accum_out=sx[:, c : c + 1])
+            nc.scalar.mul(out=sneg[:], in_=sx[:], mul=-1.0 / T)
+            for c in range(ns):
+                junk = junkp.tile([P, T], BF16, name="junk")
+                nc.scalar.activation(
+                    out=junk[:], in_=raw[:, 1, NT - ns + c, :], func=ACT.Square, bias=sneg[:, c : c + 1], accum_out=spt[:, c : c + 1]
+                )
+
         def centre(h, extra):
             raw = hd[h]["raw"]
+            nv = 2 * NT - SKT[h]
             stv = hd[h]["st"][:].rearrange("p t b (e f) -> p t (b e) f", f=3)
-            sm = statp.tile([P, 2 * NT], F32, name="sm")
+            sm = statp.tile([P, nv], F32, name="sm")
             nc.vector.tensor_reduce(out=sm[:], in_=stv[:, :, :, 1], axis=AX.X, op=ALU.add)
-            negm = statp.tile([P, 2 * NT], F32, name="negm")
+            negm = statp.tile([P, nv], F32, name="negm")
             nc.vector.tensor_scalar(out=negm[:], in0=sm[:], scalar1=-0.25, scalar2=None, op0=ALU.mult)
             xc = xcp.tile([P, 2, NT, T], BF16, name="xc")
             hd[h]["xc"] = xc
-            dd = statp.tile([P, 2 * NT, 4], F32, name="dd")
-            pt = statp.tile([P, 2 * NT], F32, name="pt")
+            dd = statp.tile([P, nv, 4], F32, name="dd")
+            pt = statp.tile([P, nv], F32, name="pt")
             hd[h]["pt"] = pt
             small = [
                 lambda: nc.vector.tensor_tensor(
-                    out=dd[:], in0=stv[:, :, :, 1], in1=negm[:].unsqueeze(2).to_broadcast([P, 2 * NT, 4]), op=ALU.add
+                    out=dd[:], in0=stv[:, :, :, 1], in1=negm[:].unsqueeze(2).to_broadcast([P, nv, 4]), op=ALU.add
                 ),
                 lambda: nc.vector.tensor_tensor(out=dd[:], in0=dd[:], in1=dd[:], op=ALU.mult),
                 lambda: nc.vector.scalar_tensor_tensor(
@@ -109,7 +131,7 @@ def tile_entropygraph_pa_t_kernel(tc, q_t, k_t, out):
                 nc.vector.tensor_scalar(
                     out=xc[:, c // NT, c % NT, :],
                     in0=raw[:, c // NT, c % NT, :],
-                    scalar1=negm[:, c : c + 1],
+                    scalar1=negm[:, c : c + 1] if c < nv else hd[h]["sneg"][:, c - nv : c - nv + 1],
                     scalar2=None,
                     op0=ALU.add,
                 )
@@ -135,8 +157,11 @@ def tile_entropygraph_pa_t_kernel(tc, q_t, k_t, out):
         def bcast(h):
             stb = stp.tile([P, NS], F32, name="stb")
             hd[h]["stb"] = stb
-            for nt in range(4):
-                nc.tensor.transpose(stb[:, P * nt : P * (nt + 1)], hd[h]["pt"][:, 4 + nt : 5 + nt].to_broadcast([P, P]), ident_f[:])
+            nv = 2 * NT - SKT[h]
+            for nt in range(NT):
+                c = NT + nt
+                col = hd[h]["pt"][:, c : c + 1] if c < nv else hd[h]["spt"][:, c - nv : c - nv + 1]
+                nc.tensor.transpose(stb[:, P * nt : P * (nt + 1)], col.to_broadcast([P, P]), ident_f[:])
 
         def rsq(h):
             s = sp.tile([P, 4, NS], F32, name="s")
@@ -234,6 +259,7 @@ def tile_entropygraph_pa_t_kernel(tc, q_t, k_t, out):
                     finish(i - 2, False)
                 if i >= -1:
                     tco(i + 1, False)
+                statsc(i + 2)
                 if i >= 1 and i % 2 == 0:
                     ln(i - 1)
                 if i >= 0:

@@ -19,6 +19,7 @@ P = 128
 NT = 4
 HALF = 512
 EPS = 1e-6
+NORM = 2.0**-40
 TAIL = "A"
 SG = 1
 SGT = 0
@@ -49,9 +50,8 @@ def tile_entropygraph_pa_t_kernel(tc, q_t, k_t, out):
         nc.vector.memset(one[:], 1.0)
         c1 = const.tile([P, 1], F32, name="c1")
         nc.vector.tensor_scalar(out=c1[:], in0=one[:], scalar1=EPS, scalar2=None, op0=ALU.add)
-        cst = const.tile([P, 2, 4], F32, name="cst")
-        nc.vector.tensor_scalar(out=cst[:, 0, :], in0=one[:].to_broadcast([P, 4]), scalar1=T * EPS, scalar2=None, op0=ALU.mult)
-        nc.vector.tensor_scalar(out=cst[:, 1, :], in0=one[:].to_broadcast([P, 4]), scalar1=-1.0 / T, scalar2=None, op0=ALU.mult)
+        ceps = const.tile([P, 1], F32, name="ceps")
+        nc.vector.tensor_scalar(out=ceps[:], in0=one[:], scalar1=EPS * NORM, scalar2=None, op0=ALU.mult)
 
         hd = [dict() for h in range(H)]
 
@@ -100,14 +100,22 @@ def tile_entropygraph_pa_t_kernel(tc, q_t, k_t, out):
                     out=junk[:], in_=raw[:, 1, NT - ns + c, :], func=ACT.Square, bias=sneg[:, c : c + 1], accum_out=spt[:, c : c + 1]
                 )
 
-        def centre(h, extra):
-            raw = hd[h]["raw"]
+        def means(h):
             nv = 2 * NT - SKT[h]
             stv = hd[h]["st"][:].rearrange("p t b (e f) -> p t (b e) f", f=3)
             sm = statp.tile([P, nv], F32, name="sm")
-            nc.vector.tensor_reduce(out=sm[:], in_=stv[:, :, :, 1], axis=AX.X, op=ALU.add)
             negm = statp.tile([P, nv], F32, name="negm")
-            nc.vector.tensor_scalar(out=negm[:], in0=sm[:], scalar1=-0.25, scalar2=None, op0=ALU.mult)
+            hd[h]["negm"] = negm
+            return [
+                lambda: nc.vector.tensor_reduce(out=sm[:], in_=stv[:, :, :, 1], axis=AX.X, op=ALU.add),
+                lambda: nc.vector.tensor_scalar(out=negm[:], in0=sm[:], scalar1=-0.25, scalar2=None, op0=ALU.mult),
+            ]
+
+        def centre(h):
+            raw = hd[h]["raw"]
+            negm = hd[h]["negm"]
+            nv = 2 * NT - SKT[h]
+            stv = hd[h]["st"][:].rearrange("p t b (e f) -> p t (b e) f", f=3)
             xc = xcp.tile([P, 2, NT, T], BF16, name="xc")
             hd[h]["xc"] = xc
             dd = statp.tile([P, nv, 4], F32, name="dd")
@@ -117,17 +125,12 @@ def tile_entropygraph_pa_t_kernel(tc, q_t, k_t, out):
                 lambda: nc.vector.tensor_tensor(
                     out=dd[:], in0=stv[:, :, :, 1], in1=negm[:].unsqueeze(2).to_broadcast([P, nv, 4]), op=ALU.add
                 ),
-                lambda: nc.vector.tensor_tensor(out=dd[:], in0=dd[:], in1=dd[:], op=ALU.mult),
                 lambda: nc.vector.scalar_tensor_tensor(
-                    out=dd[:], in0=dd[:], scalar=T / 4.0, in1=stv[:, :, :, 2], op0=ALU.mult, op1=ALU.add
+                    out=stv[:, :, :, 0], in0=dd[:], scalar=T / 4.0, in1=dd[:], op0=ALU.mult, op1=ALU.mult
                 ),
-                lambda: nc.vector.tensor_reduce(out=pt[:], in_=dd[:], axis=AX.X, op=ALU.add),
+                lambda: nc.vector.tensor_reduce(out=pt[:], in_=stv[:, :, :, 0:3:2], axis=AX.XY, op=ALU.add),
             ]
-            both = []
-            for n in range(max(len(small), len(extra))):
-                both.extend(extra[n : n + 1])
-                both.extend(small[n : n + 1])
-            for c in range(2 * NT):
+            for k, c in enumerate(range(2 * NT) if h < 2 else reversed(range(2 * NT))):
                 nc.vector.tensor_scalar(
                     out=xc[:, c // NT, c % NT, :],
                     in0=raw[:, c // NT, c % NT, :],
@@ -135,24 +138,12 @@ def tile_entropygraph_pa_t_kernel(tc, q_t, k_t, out):
                     scalar2=None,
                     op0=ALU.add,
                 )
-                run(both[c : c + 1])
-            run(both[2 * NT :])
+                run(small[k : k + 1])
 
         def sel(h):
-            pt = hd[h]["pt"]
-            kap = statp.tile([P, 4], F32, name="kap")
-            sc = statp.tile([P, 4], F32, name="sc")
-            bl = statp.tile([P, 2, 4], F32, name="bl", bufs=4)
+            sc = statp.tile([P, NT], F32, name="sc")
             hd[h]["sc"] = sc
-            hd[h]["bl"] = bl
-            return [
-                lambda: nc.vector.tensor_scalar(out=kap[:], in0=pt[:, 0:4], scalar1=T * EPS, scalar2=None, op0=ALU.max),
-                lambda: nc.vector.reciprocal(out=kap[:], in_=kap[:]),
-                lambda: nc.vector.scalar_tensor_tensor(
-                    out=sc[:], in0=pt[:, 0:4], scalar=1.0 / T, in1=kap[:], op0=ALU.mult, op1=ALU.mult
-                ),
-                lambda: nc.vector.tensor_tensor(out=bl[:], in0=kap[:].unsqueeze(1).to_broadcast([P, 2, 4]), in1=cst[:], op=ALU.mult),
-            ]
+            nc.gpsimd.tensor_scalar(out=sc[:], in0=hd[h]["pt"][:, 0:NT], scalar1=NORM / (T * T), scalar2=0.0, op0=ALU.mult, op1=ALU.add)
 
         def bcast(h):
             stb = stp.tile([P, NS], F32, name="stb")
@@ -171,7 +162,7 @@ def tile_entropygraph_pa_t_kernel(tc, q_t, k_t, out):
                     out=s[:, mt, :],
                     in_=hd[h]["stb"][:],
                     func=ACT.Abs_reciprocal_sqrt,
-                    bias=hd[h]["bl"][:, 0, mt : mt + 1],
+                    bias=ceps[:],
                     scale=hd[h]["sc"][:, mt : mt + 1],
                 )
 
@@ -194,13 +185,17 @@ def tile_entropygraph_pa_t_kernel(tc, q_t, k_t, out):
                         else:
                             nc.scalar.copy(out=dst, in_=src)
 
-        def quant(h):
+        def quant(h, between):
             grp = hd[h]["grp"]
             codes = cdp.tile([P, 2, 2, NS], U32, name="codes", align_bytes=64)
             scl = cdp.tile([P, 2, 2, NS], U8, name="scl", align_bytes=64)
             for g in range(2):
-                for o in range(2):
-                    nc.vector.quantize_mx(out=codes[:, g, o, :].bitcast(FP8X4), scales=scl[:, g, o, :], in_=grp[:, g, o, :])
+                nc.vector.quantize_mx(
+                    out=codes[:, g, :, :].rearrange("p o n -> p (o n)").bitcast(FP8X4),
+                    scales=scl[:, g, :, :].rearrange("p o n -> p (o n)"),
+                    in_=grp[:, g, :, :].rearrange("p o n -> p (o n)"),
+                )
+                run(between[g : g + 1])
             accs = [bank.tile([P, NS], F32, name="acc", tag="bank") for mt in range(4)]
             hd[h]["acc"] = accs
             for g in range(2):
@@ -233,8 +228,9 @@ def tile_entropygraph_pa_t_kernel(tc, q_t, k_t, out):
 
         def ln(h):
             t = hd[h]["t"]
-            for mt in range(4):
-                nc.scalar.activation(out=t[:, mt, :], in_=t[:, mt, :], func=ACT.Ln, bias=c1[:], scale=hd[h]["bl"][:, 1, mt : mt + 1])
+            for half in range(2):
+                sl = t[:, 2 * half : 2 * half + 2, :]
+                nc.scalar.activation(out=sl, in_=sl, func=ACT.Ln, bias=c1[:], scale=-NORM / (T * T))
 
         def finish(h, on_vector):
             t = hd[h]["t"]
@@ -266,11 +262,15 @@ def tile_entropygraph_pa_t_kernel(tc, q_t, k_t, out):
                     rsq(i)
                 if i >= 1 and i % 2 == 1:
                     ln(i - 1)
+                if i >= -1:
+                    sel(i + 1)
                 stats(i + 2)
-                extra = sel(i + 1) if i >= -1 else []
+                ms = means(i + 2)
                 if i >= 0:
-                    quant(i)
-                centre(i + 2, extra)
+                    quant(i, ms)
+                else:
+                    run(ms)
+                centre(i + 2)
                 if i >= -1:
                     bcast(i + 1)
             corr(H - 3, nc.gpsimd, SGT)
@@ -278,18 +278,18 @@ def tile_entropygraph_pa_t_kernel(tc, q_t, k_t, out):
             tco(H - 1, True)
             if TAIL == "A":
                 ln(H - 3)
-            quant(H - 2)
-            run(sel(H - 1))
+            quant(H - 2, [])
+            sel(H - 1)
             if TAIL == "D":
                 rsq(H - 2)
-                quant(H - 1)
+                quant(H - 1, [])
                 bcast(H - 1)
                 rsq(H - 1)
             else:
                 bcast(H - 1)
                 rsq(H - 2)
                 rsq(H - 1)
-                quant(H - 1)
+                quant(H - 1, [])
             if TAIL == "A":
                 finish(H - 3, False)
             corr(H - 2, nc.gpsimd, SGT)

@@ -21,7 +21,7 @@ HALF = 512
 EPS = 1e-6
 NORM = 2.0**-40
 TAIL = "A"
-SG = 1
+SG = 0
 SGT = 0
 SGT7 = 0
 F6V = 1

@@ -20,11 +20,21 @@ NT = 4
 HALF = 512
 EPS = 1e-6
 NORM = 2.0**-40
-TAIL = "A"
-SG = 0
-SGT = 0
-SGT7 = 0
-F6V = 1
+NB = 7
+NSTB = 1
+GRP = 2
+HALF_FIRST = 0
+HALF_V = 0
+SQ_S = 0
+SBUFS = 2
+AHEAD = 0
+PAR = 1
+RSQ7_FIRST = 0
+TSHARE = False
+FIN4 = 1
+SQ6S = 4
+SQ7S = 2
+LW = 1
 SKT = (3, 3, 2, 1, 1, 1, 1, 1)
 FLOPS = 2 * H * NS * NS * T
 
@@ -38,11 +48,11 @@ def tile_entropygraph_pa_t_kernel(tc, q_t, k_t, out):
         grpp = ctx.enter_context(tc.tile_pool(name="grpp", bufs=2))
         cdp = ctx.enter_context(tc.tile_pool(name="cdp", bufs=2))
         statp = ctx.enter_context(tc.tile_pool(name="statp", bufs=2))
-        sp = ctx.enter_context(tc.tile_pool(name="sp", bufs=2))
+        sp = ctx.enter_context(tc.tile_pool(name="sp", bufs=SBUFS))
         junkp = ctx.enter_context(tc.tile_pool(name="junkp", bufs=2))
         tpl = ctx.enter_context(tc.tile_pool(name="tpl", bufs=4))
-        bank = ctx.enter_context(tc.psum_pool(name="bank", bufs=7))
-        stp = ctx.enter_context(tc.psum_pool(name="stp", bufs=1))
+        bank = ctx.enter_context(tc.psum_pool(name="bank", bufs=NB))
+        stp = ctx.enter_context(tc.psum_pool(name="stp", bufs=NSTB))
 
         ident_f = const.tile([P, P], F32, name="ident_f")
         make_identity(nc, ident_f[:])
@@ -141,7 +151,7 @@ def tile_entropygraph_pa_t_kernel(tc, q_t, k_t, out):
                 run(small[k : k + 1])
 
         def sel(h):
-            sc = statp.tile([P, NT], F32, name="sc")
+            sc = statp.tile([P, NT], F32, name="sc", bufs=4)
             hd[h]["sc"] = sc
             nc.gpsimd.tensor_scalar(out=sc[:], in0=hd[h]["pt"][:, 0:NT], scalar1=NORM / (T * T), scalar2=0.0, op0=ALU.mult, op1=ALU.add)
 
@@ -210,38 +220,55 @@ def tile_entropygraph_pa_t_kernel(tc, q_t, k_t, out):
                         stop=(g == 1),
                     )
 
-        def corr(h, square_on, sg):
-            t = tpl.tile([P, 4, NS], F32, name="t")
-            hd[h]["t"] = t
-            s = hd[h]["s"]
-            for mt in range(4):
-                if mt >= 4 - sg:
-                    nc.scalar.activation(out=t[:, mt, :], in_=hd[h]["acc"][mt][:], func=ACT.Square)
-                else:
-                    nc.vector.tensor_tensor(out=t[:, mt, :], in0=hd[h]["acc"][mt][:], in1=s[:, mt, :], op=ALU.mult)
-            for mt in range(4):
-                if mt >= 4 - sg:
-                    square_on.tensor_tensor(out=t[:, mt, :], in0=t[:, mt, :], in1=s[:, mt, :], op=ALU.mult)
-                    square_on.tensor_tensor(out=t[:, mt, :], in0=t[:, mt, :], in1=s[:, mt, :], op=ALU.mult)
-                else:
-                    square_on.tensor_tensor(out=t[:, mt, :], in0=t[:, mt, :], in1=t[:, mt, :], op=ALU.mult)
+        def corr(h, mts=range(4)):
+            if "t" not in hd[h]:
+                t = tpl.tile([P, 4, NS], F32, name="t")
+                hd[h]["t"] = t
+            for mt in mts:
+                nc.vector.tensor_tensor(out=hd[h]["t"][:, mt, :], in0=hd[h]["acc"][mt][:], in1=hd[h]["s"][:, mt, :], op=ALU.mult)
 
-        def ln(h):
-            t = hd[h]["t"]
-            for half in range(2):
-                sl = t[:, 2 * half : 2 * half + 2, :]
+        def square(h, eng, mts=range(4)):
+            for mt in mts:
+                sl = hd[h]["t"][:, mt, :]
+                if eng is nc.scalar:
+                    nc.scalar.activation(out=sl, in_=sl, func=ACT.Square)
+                else:
+                    eng.tensor_tensor(out=sl, in0=sl, in1=sl, op=ALU.mult)
+
+        def ln(h, w=2):
+            for a in range(0, 4, w):
+                sl = hd[h]["t"][:, a : a + w, :]
                 nc.scalar.activation(out=sl, in_=sl, func=ACT.Ln, bias=c1[:], scale=-NORM / (T * T))
 
-        def finish(h, on_vector):
+        def finish(h, on_vector, w=2):
             t = hd[h]["t"]
             ov = out[0, h, :, :].rearrange("(mt m) j -> m mt j", m=P)
-            for half in range(2):
-                sl = t[:, 2 * half : 2 * half + 2, :]
+            for a in range(0, 4, w):
+                sl = t[:, a : a + w, :]
                 if on_vector:
                     nc.vector.tensor_scalar(out=sl, in0=sl, scalar1=-0.5, scalar2=None, op0=ALU.mult)
                 else:
                     nc.gpsimd.tensor_scalar(out=sl, in0=sl, scalar1=-0.5, scalar2=0.0, op0=ALU.mult, op1=ALU.add)
-                nc.sync.dma_start(out=ov[:, 2 * half : 2 * half + 2, :], in_=sl)
+                nc.sync.dma_start(out=ov[:, a : a + w, :], in_=sl)
+
+        def roots_logs(i):
+            k = i % 3
+            if k == 2:
+                order = [("l", i - 1), ("r", i), ("r", i + 1)]
+            elif k == 0:
+                order = [("r", i + 1), ("l", i - 1)]
+            else:
+                order = [("l", i - 1)]
+            if GRP == 2:
+                order = [("r", i + AHEAD), ("l", i - 1)] if (i + PAR) % 2 else [("l", i - 1), ("r", i + AHEAD)]
+            for kind, h in order:
+                if kind == "r" and 0 <= h < H:
+                    if "stb" not in hd[h]:
+                        bcast(h)
+                    rsq(h)
+                if kind == "l" and 0 <= h < H - 3:
+                    square(h, nc.scalar, range(4 - SQ_S, 4))
+                    ln(h)
 
         with tc.manual_schedule():
             for h in range(3):
@@ -250,54 +277,61 @@ def tile_entropygraph_pa_t_kernel(tc, q_t, k_t, out):
                 if i >= -1 and i + 4 < H:
                     load(i + 4)
                 if i >= 1:
-                    corr(i - 1, nc.gpsimd, SG)
-                if i >= 2:
-                    finish(i - 2, False)
+                    corr(i - 1)
+                    if HALF_FIRST and i >= 2:
+                        finish(i - 2, HALF_V)
+                    square(i - 1, nc.gpsimd, range(4 - SQ_S))
+                    if not HALF_FIRST and not HALF_V and i >= 2:
+                        finish(i - 2, False)
                 if i >= -1:
                     tco(i + 1, False)
                 statsc(i + 2)
-                if i >= 1 and i % 2 == 0:
-                    ln(i - 1)
-                if i >= 0:
-                    rsq(i)
-                if i >= 1 and i % 2 == 1:
-                    ln(i - 1)
-                if i >= -1:
-                    sel(i + 1)
+                roots_logs(i)
                 stats(i + 2)
                 ms = means(i + 2)
                 if i >= 0:
                     quant(i, ms)
                 else:
                     run(ms)
+                if HALF_V and not HALF_FIRST and i >= 2:
+                    finish(i - 2, True)
                 centre(i + 2)
-                if i >= -1:
-                    bcast(i + 1)
-            corr(H - 3, nc.gpsimd, SGT)
-            finish(H - 4, False)
-            tco(H - 1, True)
-            if TAIL == "A":
-                ln(H - 3)
-            quant(H - 2, [])
-            sel(H - 1)
-            if TAIL == "D":
-                rsq(H - 2)
-                quant(H - 1, [])
-                bcast(H - 1)
-                rsq(H - 1)
-            else:
-                bcast(H - 1)
-                rsq(H - 2)
-                rsq(H - 1)
-                quant(H - 1, [])
-            if TAIL == "A":
-                finish(H - 3, False)
-            corr(H - 2, nc.gpsimd, SGT)
-            corr(H - 1, nc.vector, SGT7)
-            if TAIL != "A":
-                ln(H - 3)
-                finish(H - 3, False)
-            ln(H - 2)
-            finish(H - 2, F6V == 1)
-            ln(H - 1)
-            finish(H - 1, True)
+                sel(i + 2)
+                if NSTB > 1:
+                    bcast(i + 2)
+            L = H - 1
+            corr(L - 2)
+            if "stb" not in hd[L]:
+                if "stb" not in hd[L - 1]:
+                    bcast(L - 1)
+                    rsq(L - 1)
+                bcast(L)
+            elif "s" not in hd[L - 1]:
+                rsq(L - 1)
+            if RSQ7_FIRST:
+                rsq(L)
+            tco(L, TSHARE)
+            quant(L - 1, [])
+            square(L - 2, nc.vector)
+            if not RSQ7_FIRST:
+                rsq(L)
+            if FIN4 == 0:
+                finish(L - 3, True)
+            ln(L - 2)
+            quant(L, [])
+            if FIN4 == 1:
+                finish(L - 3, True)
+            corr(L - 1)
+            for mt in range(4 - SQ6S):
+                square(L - 1, nc.vector, [mt])
+            if SQ6S:
+                square(L - 1, nc.scalar, range(4 - SQ6S, 4))
+            ln(L - 1)
+            corr(L)
+            square(L, nc.vector, range(0, 4 - SQ7S))
+            if SQ7S:
+                square(L, nc.scalar, range(4 - SQ7S, 4))
+            finish(L - 2, True)
+            ln(L, LW)
+            finish(L - 1, True)
+            finish(L, True, LW)

@@ -26,16 +26,17 @@ GRP = 2
 HALF_FIRST = 0
 HALF_V = 0
 SQ_S = 0
-SBUFS = 2
-AHEAD = 0
-PAR = 1
+SBUFS = 3
+SFIRST = 1
+AHEAD = 1
+PAR = 0
 RSQ7_FIRST = 0
 TSHARE = False
 FIN4 = 1
 SQ6S = 4
 SQ7S = 2
 LW = 1
-SKT = (3, 3, 2, 1, 1, 1, 1, 1)
+SKT = (2, 2, 1, 1, 1, 1, 1, 1)
 FLOPS = 2 * H * NS * NS * T
 
 
@@ -283,10 +284,21 @@ def tile_entropygraph_pa_t_kernel(tc, q_t, k_t, out):
                     square(i - 1, nc.gpsimd, range(4 - SQ_S))
                     if not HALF_FIRST and not HALF_V and i >= 2:
                         finish(i - 2, False)
-                if i >= -1:
+                if not SFIRST and i >= -1:
                     tco(i + 1, False)
                 statsc(i + 2)
-                roots_logs(i)
+                if SFIRST == 2 and (i + PAR) % 2:
+                    if 0 <= i + AHEAD < H:
+                        bcast(i + AHEAD)
+                        rsq(i + AHEAD)
+                    if i >= -1:
+                        tco(i + 1, False)
+                    if i >= 1:
+                        ln(i - 1)
+                else:
+                    if SFIRST and i >= -1:
+                        tco(i + 1, False)
+                    roots_logs(i)
                 stats(i + 2)
                 ms = means(i + 2)
                 if i >= 0:

@@ -20,14 +20,18 @@ NT = 4
 HALF = 512
 EPS = 1e-6
 NORM = 2.0**-40
-NB = 7
-NSTB = 1
-GRP = 2
+NB = 6
+NSTB = 2
+GRP = 3
 HALF_FIRST = 0
 HALF_V = 0
 SQ_S = 0
 SBUFS = 3
-SFIRST = 1
+NQ = 0
+GD4 = 0
+GD5 = 1
+PH = 2
+SFIRST = 0
 AHEAD = 1
 PAR = 0
 RSQ7_FIRST = 0
@@ -176,6 +180,9 @@ def tile_entropygraph_pa_t_kernel(tc, q_t, k_t, out):
                     bias=ceps[:],
                     scale=hd[h]["sc"][:, mt : mt + 1],
                 )
+            if NQ and h < H - 3:
+                sl = s[:, 4 - NQ : 4, :]
+                nc.scalar.activation(out=sl, in_=sl, func=ACT.Square)
 
         def tco(h, share):
             xc = hd[h]["xc"]
@@ -226,12 +233,17 @@ def tile_entropygraph_pa_t_kernel(tc, q_t, k_t, out):
                 t = tpl.tile([P, 4, NS], F32, name="t")
                 hd[h]["t"] = t
             for mt in mts:
-                nc.vector.tensor_tensor(out=hd[h]["t"][:, mt, :], in0=hd[h]["acc"][mt][:], in1=hd[h]["s"][:, mt, :], op=ALU.mult)
+                if mt >= 4 - NQ and h < H - 3:
+                    nc.scalar.activation(out=hd[h]["t"][:, mt, :], in_=hd[h]["acc"][mt][:], func=ACT.Square)
+                else:
+                    nc.vector.tensor_tensor(out=hd[h]["t"][:, mt, :], in0=hd[h]["acc"][mt][:], in1=hd[h]["s"][:, mt, :], op=ALU.mult)
 
         def square(h, eng, mts=range(4)):
             for mt in mts:
                 sl = hd[h]["t"][:, mt, :]
-                if eng is nc.scalar:
+                if mt >= 4 - NQ and h < H - 3:
+                    eng.tensor_tensor(out=sl, in0=sl, in1=hd[h]["s"][:, mt, :], op=ALU.mult)
+                elif eng is nc.scalar:
                     nc.scalar.activation(out=sl, in_=sl, func=ACT.Square)
                 else:
                     eng.tensor_tensor(out=sl, in0=sl, in1=sl, op=ALU.mult)
@@ -252,24 +264,29 @@ def tile_entropygraph_pa_t_kernel(tc, q_t, k_t, out):
                     nc.gpsimd.tensor_scalar(out=sl, in0=sl, scalar1=-0.5, scalar2=0.0, op0=ALU.mult, op1=ALU.add)
                 nc.sync.dma_start(out=ov[:, a : a + w, :], in_=sl)
 
-        def roots_logs(i):
-            k = i % 3
-            if k == 2:
-                order = [("l", i - 1), ("r", i), ("r", i + 1)]
-            elif k == 0:
-                order = [("r", i + 1), ("l", i - 1)]
-            else:
-                order = [("l", i - 1)]
-            if GRP == 2:
-                order = [("r", i + AHEAD), ("l", i - 1)] if (i + PAR) % 2 else [("l", i - 1), ("r", i + AHEAD)]
-            for kind, h in order:
-                if kind == "r" and 0 <= h < H:
-                    if "stb" not in hd[h]:
-                        bcast(h)
-                    rsq(h)
-                if kind == "l" and 0 <= h < H - 3:
-                    square(h, nc.scalar, range(4 - SQ_S, 4))
-                    ln(h)
+        def root(h):
+            if 0 <= h < H:
+                if "stb" not in hd[h]:
+                    bcast(h)
+                rsq(h)
+
+        def scalar_turn(i):
+            k = (i + PH) % GRP
+            statsc(i + 2)
+            if k == 0 and AHEAD:
+                root(i + 1)
+            if i >= -1:
+                tco(i + 1, False)
+            if k == 0 and not AHEAD:
+                root(i + 1)
+            if 1 <= i:
+                if SQ_S:
+                    square(i - 1, nc.scalar, range(4 - SQ_S, 4))
+                ln(i - 1)
+            if k == GRP - 1:
+                if GRP == 3:
+                    root(i)
+                root(i + 1)
 
         with tc.manual_schedule():
             for h in range(3):
@@ -284,21 +301,7 @@ def tile_entropygraph_pa_t_kernel(tc, q_t, k_t, out):
                     square(i - 1, nc.gpsimd, range(4 - SQ_S))
                     if not HALF_FIRST and not HALF_V and i >= 2:
                         finish(i - 2, False)
-                if not SFIRST and i >= -1:
-                    tco(i + 1, False)
-                statsc(i + 2)
-                if SFIRST == 2 and (i + PAR) % 2:
-                    if 0 <= i + AHEAD < H:
-                        bcast(i + AHEAD)
-                        rsq(i + AHEAD)
-                    if i >= -1:
-                        tco(i + 1, False)
-                    if i >= 1:
-                        ln(i - 1)
-                else:
-                    if SFIRST and i >= -1:
-                        tco(i + 1, False)
-                    roots_logs(i)
+                scalar_turn(i)
                 stats(i + 2)
                 ms = means(i + 2)
                 if i >= 0:
@@ -313,6 +316,8 @@ def tile_entropygraph_pa_t_kernel(tc, q_t, k_t, out):
                     bcast(i + 2)
             L = H - 1
             corr(L - 2)
+            if GD4:
+                finish(L - 3, False)
             if "stb" not in hd[L]:
                 if "stb" not in hd[L - 1]:
                     bcast(L - 1)
@@ -327,12 +332,14 @@ def tile_entropygraph_pa_t_kernel(tc, q_t, k_t, out):
             square(L - 2, nc.vector)
             if not RSQ7_FIRST:
                 rsq(L)
-            if FIN4 == 0:
-                finish(L - 3, True)
+            if not GD4 and FIN4 == 0:
+                finish(L - 3, not GD4)
             ln(L - 2)
             quant(L, [])
-            if FIN4 == 1:
-                finish(L - 3, True)
+            if not GD4 and FIN4 == 1:
+                finish(L - 3, not GD4)
+            if GD5:
+                finish(L - 2, False)
             corr(L - 1)
             for mt in range(4 - SQ6S):
                 square(L - 1, nc.vector, [mt])
@@ -343,7 +350,8 @@ def tile_entropygraph_pa_t_kernel(tc, q_t, k_t, out):
             square(L, nc.vector, range(0, 4 - SQ7S))
             if SQ7S:
                 square(L, nc.scalar, range(4 - SQ7S, 4))
-            finish(L - 2, True)
+            if not GD5:
+                finish(L - 2, True)
             ln(L, LW)
             finish(L - 1, True)
             finish(L, True, LW)

@@ -40,7 +40,7 @@ FIN4 = 1
 SQ6S = 4
 SQ7S = 2
 LW = 1
-SKT = (2, 2, 1, 1, 1, 1, 1, 1)
+SKT = (3, 2, 1, 1, 1, 1, 1, 1)
 FLOPS = 2 * H * NS * NS * T
 
 
@@ -77,14 +77,16 @@ def tile_entropygraph_pa_t_kernel(tc, q_t, k_t, out):
         def load(h):
             raw = rawp.tile([P, 2, NT, T], BF16, name="raw")
             hd[h]["raw"] = raw
-            cuts = ((0, 1), (1, 2), (2, NT)) if h == 0 else ((0, NT),)
-            for o in range(2):
-                src = (q_t, k_t)[o]
-                for a0, a1 in cuts:
-                    nc.sync.dma_start(
-                        out=raw[:, o, a0:a1, :],
-                        in_=src[0, h, P * a0 : P * a1, o : o + T].rearrange("(a p) k -> p a k", p=P),
-                    )
+            if h == 0:
+                nk = NT - SKT[0]
+                pieces = [(0, 0, 1, 0, HALF), (0, 0, 1, HALF, T), (0, 1, 2, 0, T), (0, 2, NT, 0, T), (1, 0, 1, 0, T), (1, 1, 2, 0, T), (1, 2, NT, 0, T)]
+            else:
+                pieces = [(0, 0, NT, 0, T), (1, 0, NT, 0, T)]
+            for o, a0, a1, k0, k1 in pieces:
+                nc.sync.dma_start(
+                    out=raw[:, o, a0:a1, k0:k1],
+                    in_=(q_t, k_t)[o][0, h, P * a0 : P * a1, o + k0 : o + k1].rearrange("(a p) k -> p a k", p=P),
+                )
 
         def stats(h):
             raw = hd[h]["raw"]
@@ -97,18 +99,21 @@ def tile_entropygraph_pa_t_kernel(tc, q_t, k_t, out):
                         out=st[:, c, half, :], in_=raw[:, c // NT, c % NT, HALF * half : HALF * (half + 1)]
                     )
 
-        def statsc(h):
+        def sums(h):
             raw = hd[h]["raw"]
             ns = SKT[h]
-            sx = statp.tile([P, ns], F32, name="sx")
             sneg = statp.tile([P, ns], F32, name="sneg")
             spt = statp.tile([P, ns], F32, name="spt")
             hd[h]["sneg"] = sneg
             hd[h]["spt"] = spt
             for c in range(ns):
                 junk = junkp.tile([P, T], BF16, name="junk")
-                nc.scalar.activation(out=junk[:], in_=raw[:, 1, NT - ns + c, :], func=ACT.Copy, accum_out=sx[:, c : c + 1])
-            nc.scalar.mul(out=sneg[:], in_=sx[:], mul=-1.0 / T)
+                nc.scalar.activation(out=junk[:], in_=raw[:, 1, NT - ns + c, :], func=ACT.Copy, scale=-1.0 / T, accum_out=sneg[:, c : c + 1])
+        def spreads(h):
+            raw = hd[h]["raw"]
+            ns = SKT[h]
+            sneg = hd[h]["sneg"]
+            spt = hd[h]["spt"]
             for c in range(ns):
                 junk = junkp.tile([P, T], BF16, name="junk")
                 nc.scalar.activation(
@@ -184,7 +189,7 @@ def tile_entropygraph_pa_t_kernel(tc, q_t, k_t, out):
                 sl = s[:, 4 - NQ : 4, :]
                 nc.scalar.activation(out=sl, in_=sl, func=ACT.Square)
 
-        def tco(h, share):
+        def tco(h, share, between=()):
             xc = hd[h]["xc"]
             grp = grpp.tile([P, 2, 2, 2048], BF16, name="grp", align_bytes=64)
             hd[h]["grp"] = grp
@@ -202,6 +207,8 @@ def tile_entropygraph_pa_t_kernel(tc, q_t, k_t, out):
                             nc.vector.tensor_copy(out=dst, in_=src)
                         else:
                             nc.scalar.copy(out=dst, in_=src)
+                        run(between)
+                        between = ()
 
         def quant(h, between):
             grp = hd[h]["grp"]
@@ -272,11 +279,13 @@ def tile_entropygraph_pa_t_kernel(tc, q_t, k_t, out):
 
         def scalar_turn(i):
             k = (i + PH) % GRP
-            statsc(i + 2)
+            sums(i + 2)
             if k == 0 and AHEAD:
                 root(i + 1)
             if i >= -1:
-                tco(i + 1, False)
+                tco(i + 1, False, [lambda: spreads(i + 2)])
+            else:
+                spreads(i + 2)
             if k == 0 and not AHEAD:
                 root(i + 1)
             if 1 <= i:

from contextlib import ExitStack

import concourse.mybir as mybir
from concourse.masks import make_identity

F32 = mybir.dt.float32
BF16 = mybir.dt.bfloat16
U32 = mybir.dt.uint32
U8 = mybir.dt.uint8
FP8X4 = mybir.dt.float8_e4m3fn_x4
ALU = mybir.AluOpType
ACT = mybir.ActivationFunctionType
AX = mybir.AxisListType

H = 8
NS = 512
T = 1024
P = 128
NT = 4
HALF = 512
EPS = 1e-6
NORM = 2.0**-40
NB = 6
NSTB = 2
GRP = 3
HALF_FIRST = 0
HALF_V = 0
SQ_S = 0
SBUFS = 3
NQ = 0
GD4 = 0
GD5 = 1
PH = 2
SFIRST = 0
AHEAD = 1
PAR = 0
RSQ7_FIRST = 0
TSHARE = False
FIN4 = 1
SQ6S = 4
SQ7S = 2
LW = 1
SKT = (3, 2, 1, 1, 1, 1, 1, 1)
FLOPS = 2 * H * NS * NS * T


def tile_entropygraph_pa_t_kernel(tc, q_t, k_t, out):
    nc = tc.nc
    with ExitStack() as ctx:
        const = ctx.enter_context(tc.tile_pool(name="const", bufs=1))
        rawp = ctx.enter_context(tc.tile_pool(name="rawp", bufs=3))
        xcp = ctx.enter_context(tc.tile_pool(name="xcp", bufs=2))
        grpp = ctx.enter_context(tc.tile_pool(name="grpp", bufs=2))
        cdp = ctx.enter_context(tc.tile_pool(name="cdp", bufs=2))
        statp = ctx.enter_context(tc.tile_pool(name="statp", bufs=2))
        sp = ctx.enter_context(tc.tile_pool(name="sp", bufs=SBUFS))
        junkp = ctx.enter_context(tc.tile_pool(name="junkp", bufs=2))
        tpl = ctx.enter_context(tc.tile_pool(name="tpl", bufs=4))
        bank = ctx.enter_context(tc.psum_pool(name="bank", bufs=NB))
        stp = ctx.enter_context(tc.psum_pool(name="stp", bufs=NSTB))

        ident_f = const.tile([P, P], F32, name="ident_f")
        make_identity(nc, ident_f[:])
        one = const.tile([P, 1], F32, name="one")
        nc.vector.memset(one[:], 1.0)
        c1 = const.tile([P, 1], F32, name="c1")
        nc.vector.tensor_scalar(out=c1[:], in0=one[:], scalar1=EPS, scalar2=None, op0=ALU.add)
        ceps = const.tile([P, 1], F32, name="ceps")
        nc.vector.tensor_scalar(out=ceps[:], in0=one[:], scalar1=EPS * NORM, scalar2=None, op0=ALU.mult)

        hd = [dict() for h in range(H)]

        def run(ops):
            for op in ops:
                op()

        def load(h):
            raw = rawp.tile([P, 2, NT, T], BF16, name="raw")
            hd[h]["raw"] = raw
            if h == 0:
                nk = NT - SKT[0]
                pieces = [(0, 0, 1, 0, HALF), (0, 0, 1, HALF, T), (0, 1, 2, 0, T), (0, 2, NT, 0, T), (1, 0, 1, 0, T), (1, 1, 2, 0, T), (1, 2, NT, 0, T)]
            else:
                pieces = [(0, 0, NT, 0, T), (1, 0, NT, 0, T)]
            for o, a0, a1, k0, k1 in pieces:
                nc.sync.dma_start(
                    out=raw[:, o, a0:a1, k0:k1],
                    in_=(q_t, k_t)[o][0, h, P * a0 : P * a1, o + k0 : o + k1].rearrange("(a p) k -> p a k", p=P),
                )

        def stats(h):
            raw = hd[h]["raw"]
            nv = 2 * NT - SKT[h]
            st = statp.tile([P, nv, 2, 6], F32, name="st")
            hd[h]["st"] = st
            for c in range(nv):
                for half in range(2):
                    nc.vector.bn_stats(
                        out=st[:, c, half, :], in_=raw[:, c // NT, c % NT, HALF * half : HALF * (half + 1)]
                    )

        def sums(h):
            raw = hd[h]["raw"]
            ns = SKT[h]
            sneg = statp.tile([P, ns], F32, name="sneg")
            spt = statp.tile([P, ns], F32, name="spt")
            hd[h]["sneg"] = sneg
            hd[h]["spt"] = spt
            for c in range(ns):
                junk = junkp.tile([P, T], BF16, name="junk")
                nc.scalar.activation(out=junk[:], in_=raw[:, 1, NT - ns + c, :], func=ACT.Copy, scale=-1.0 / T, accum_out=sneg[:, c : c + 1])
        def spreads(h):
            raw = hd[h]["raw"]
            ns = SKT[h]
            sneg = hd[h]["sneg"]
            spt = hd[h]["spt"]
            for c in range(ns):
                junk = junkp.tile([P, T], BF16, name="junk")
                nc.scalar.activation(
                    out=junk[:], in_=raw[:, 1, NT - ns + c, :], func=ACT.Square, bias=sneg[:, c : c + 1], accum_out=spt[:, c : c + 1]
                )

        def means(h):
            nv = 2 * NT - SKT[h]
            stv = hd[h]["st"][:].rearrange("p t b (e f) -> p t (b e) f", f=3)
            sm = statp.tile([P, nv], F32, name="sm")
            negm = statp.tile([P, nv], F32, name="negm")
            hd[h]["negm"] = negm
            return [
                lambda: nc.vector.tensor_reduce(out=sm[:], in_=stv[:, :, :, 1], axis=AX.X, op=ALU.add),
                lambda: nc.vector.tensor_scalar(out=negm[:], in0=sm[:], scalar1=-0.25, scalar2=None, op0=ALU.mult),
            ]

        def centre(h):
            raw = hd[h]["raw"]
            negm = hd[h]["negm"]
            nv = 2 * NT - SKT[h]
            stv = hd[h]["st"][:].rearrange("p t b (e f) -> p t (b e) f", f=3)
            xc = xcp.tile([P, 2, NT, T], BF16, name="xc")
            hd[h]["xc"] = xc
            dd = statp.tile([P, nv, 4], F32, name="dd")
            pt = statp.tile([P, nv], F32, name="pt")
            hd[h]["pt"] = pt
            small = [
                lambda: nc.vector.tensor_tensor(
                    out=dd[:], in0=stv[:, :, :, 1], in1=negm[:].unsqueeze(2).to_broadcast([P, nv, 4]), op=ALU.add
                ),
                lambda: nc.vector.scalar_tensor_tensor(
                    out=stv[:, :, :, 0], in0=dd[:], scalar=T / 4.0, in1=dd[:], op0=ALU.mult, op1=ALU.mult
                ),
                lambda: nc.vector.tensor_reduce(out=pt[:], in_=stv[:, :, :, 0:3:2], axis=AX.XY, op=ALU.add),
            ]
            for k, c in enumerate(range(2 * NT) if h < 2 else reversed(range(2 * NT))):
                nc.vector.tensor_scalar(
                    out=xc[:, c // NT, c % NT, :],
                    in0=raw[:, c // NT, c % NT, :],
                    scalar1=negm[:, c : c + 1] if c < nv else hd[h]["sneg"][:, c - nv : c - nv + 1],
                    scalar2=None,
                    op0=ALU.add,
                )
                run(small[k : k + 1])

        def sel(h):
            sc = statp.tile([P, NT], F32, name="sc", bufs=4)
            hd[h]["sc"] = sc
            nc.gpsimd.tensor_scalar(out=sc[:], in0=hd[h]["pt"][:, 0:NT], scalar1=NORM / (T * T), scalar2=0.0, op0=ALU.mult, op1=ALU.add)

        def bcast(h):
            stb = stp.tile([P, NS], F32, name="stb")
            hd[h]["stb"] = stb
            nv = 2 * NT - SKT[h]
            for nt in range(NT):
                c = NT + nt
                col = hd[h]["pt"][:, c : c + 1] if c < nv else hd[h]["spt"][:, c - nv : c - nv + 1]
                nc.tensor.transpose(stb[:, P * nt : P * (nt + 1)], col.to_broadcast([P, P]), ident_f[:])

        def rsq(h):
            s = sp.tile([P, 4, NS], F32, name="s")
            hd[h]["s"] = s
            for mt in range(4):
                nc.scalar.activation(
                    out=s[:, mt, :],
                    in_=hd[h]["stb"][:],
                    func=ACT.Abs_reciprocal_sqrt,
                    bias=ceps[:],
                    scale=hd[h]["sc"][:, mt : mt + 1],
                )
            if NQ and h < H - 3:
                sl = s[:, 4 - NQ : 4, :]
                nc.scalar.activation(out=sl, in_=sl, func=ACT.Square)

        def tco(h, share, between=()):
            xc = hd[h]["xc"]
            grp = grpp.tile([P, 2, 2, 2048], BF16, name="grp", align_bytes=64)
            hd[h]["grp"] = grp
            for g in range(2):
                for o in range(2):
                    for b in range(2):
                        tp = bank.tile([P, 2, 2, P], F32, name="tp", tag="bank")
                        for a in range(2):
                            words = xc[:, o, 2 * b + a, :].bitcast(F32)
                            for u in range(2):
                                nc.tensor.transpose(tp[:, u, a, :], words[:, 256 * g + u : 256 * (g + 1) : 2], ident_f[:])
                        dst = grp[:, g, o, 1024 * b : 1024 * (b + 1)].bitcast(F32).rearrange("p (r u) -> p r u", u=2)
                        src = tp[:].rearrange("p u a i -> p (a i) u")
                        if share and b == 1:
                            nc.vector.tensor_copy(out=dst, in_=src)
                        else:
                            nc.scalar.copy(out=dst, in_=src)
                        run(between)
                        between = ()

        def quant(h, between):
            grp = hd[h]["grp"]
            codes = cdp.tile([P, 2, 2, NS], U32, name="codes", align_bytes=64)
            scl = cdp.tile([P, 2, 2, NS], U8, name="scl", align_bytes=64)
            for g in range(2):
                nc.vector.quantize_mx(
                    out=codes[:, g, :, :].rearrange("p o n -> p (o n)").bitcast(FP8X4),
                    scales=scl[:, g, :, :].rearrange("p o n -> p (o n)"),
                    in_=grp[:, g, :, :].rearrange("p o n -> p (o n)"),
                )
                run(between[g : g + 1])
            accs = [bank.tile([P, NS], F32, name="acc", tag="bank") for mt in range(4)]
            hd[h]["acc"] = accs
            for g in range(2):
                for mt in range(4):
                    nc.tensor.matmul_mx(
                        out=accs[mt][:],
                        lhsT=codes[:, g, 0, P * mt : P * (mt + 1)].bitcast(FP8X4),
                        lhsT_scale=scl[:, g, 0, P * mt : P * (mt + 1)],
                        rhs=codes[:, g, 1, :].bitcast(FP8X4),
                        rhs_scale=scl[:, g, 1, :],
                        start=(g == 0),
                        stop=(g == 1),
                    )

        def corr(h, mts=range(4)):
            if "t" not in hd[h]:
                t = tpl.tile([P, 4, NS], F32, name="t")
                hd[h]["t"] = t
            for mt in mts:
                if mt >= 4 - NQ and h < H - 3:
                    nc.scalar.activation(out=hd[h]["t"][:, mt, :], in_=hd[h]["acc"][mt][:], func=ACT.Square)
                else:
                    nc.vector.tensor_tensor(out=hd[h]["t"][:, mt, :], in0=hd[h]["acc"][mt][:], in1=hd[h]["s"][:, mt, :], op=ALU.mult)

        def square(h, eng, mts=range(4)):
            for mt in mts:
                sl = hd[h]["t"][:, mt, :]
                if mt >= 4 - NQ and h < H - 3:
                    eng.tensor_tensor(out=sl, in0=sl, in1=hd[h]["s"][:, mt, :], op=ALU.mult)
                elif eng is nc.scalar:
                    nc.scalar.activation(out=sl, in_=sl, func=ACT.Square)
                else:
                    eng.tensor_tensor(out=sl, in0=sl, in1=sl, op=ALU.mult)

        def ln(h, w=2):
            for a in range(0, 4, w):
                sl = hd[h]["t"][:, a : a + w, :]
                nc.scalar.activation(out=sl, in_=sl, func=ACT.Ln, bias=c1[:], scale=-NORM / (T * T))

        def finish(h, on_vector, w=2):
            t = hd[h]["t"]
            ov = out[0, h, :, :].rearrange("(mt m) j -> m mt j", m=P)
            for a in range(0, 4, w):
                sl = t[:, a : a + w, :]
                if on_vector:
                    nc.vector.tensor_scalar(out=sl, in0=sl, scalar1=-0.5, scalar2=None, op0=ALU.mult)
                else:
                    nc.gpsimd.tensor_scalar(out=sl, in0=sl, scalar1=-0.5, scalar2=0.0, op0=ALU.mult, op1=ALU.add)
                nc.sync.dma_start(out=ov[:, a : a + w, :], in_=sl)

        def root(h):
            if 0 <= h < H:
                if "stb" not in hd[h]:
                    bcast(h)
                rsq(h)

        def scalar_turn(i):
            k = (i + PH) % GRP
            sums(i + 2)
            if k == 0 and AHEAD:
                root(i + 1)
            if i >= -1:
                tco(i + 1, False, [lambda: spreads(i + 2)])
            else:
                spreads(i + 2)
            if k == 0 and not AHEAD:
                root(i + 1)
            if 1 <= i:
                if SQ_S:
                    square(i - 1, nc.scalar, range(4 - SQ_S, 4))
                ln(i - 1)
            if k == GRP - 1:
                if GRP == 3:
                    root(i)
                root(i + 1)

        with tc.manual_schedule():
            for h in range(3):
                load(h)
            for i in range(-2, H - 2):
                if i >= -1 and i + 4 < H:
                    load(i + 4)
                if i >= 1:
                    corr(i - 1)
                    if HALF_FIRST and i >= 2:
                        finish(i - 2, HALF_V)
                    square(i - 1, nc.gpsimd, range(4 - SQ_S))
                    if not HALF_FIRST and not HALF_V and i >= 2:
                        finish(i - 2, False)
                scalar_turn(i)
                stats(i + 2)
                ms = means(i + 2)
                if i >= 0:
                    quant(i, ms)
                else:
                    run(ms)
                if HALF_V and not HALF_FIRST and i >= 2:
                    finish(i - 2, True)
                centre(i + 2)
                sel(i + 2)
                if NSTB > 1:
                    bcast(i + 2)
            L = H - 1
            corr(L - 2)
            if GD4:
                finish(L - 3, False)
            if "stb" not in hd[L]:
                if "stb" not in hd[L - 1]:
                    bcast(L - 1)
                    rsq(L - 1)
                bcast(L)
            elif "s" not in hd[L - 1]:
                rsq(L - 1)
            if RSQ7_FIRST:
                rsq(L)
            tco(L, TSHARE)
            quant(L - 1, [])
            square(L - 2, nc.vector)
            if not RSQ7_FIRST:
                rsq(L)
            if not GD4 and FIN4 == 0:
                finish(L - 3, not GD4)
            ln(L - 2)
            quant(L, [])
            if not GD4 and FIN4 == 1:
                finish(L - 3, not GD4)
            if GD5:
                finish(L - 2, False)
            corr(L - 1)
            for mt in range(4 - SQ6S):
                square(L - 1, nc.vector, [mt])
            if SQ6S:
                square(L - 1, nc.scalar, range(4 - SQ6S, 4))
            ln(L - 1)
            corr(L)
            square(L, nc.vector, range(0, 4 - SQ7S))
            if SQ7S:
                square(L, nc.scalar, range(4 - SQ7S, 4))
            if not GD5:
                finish(L - 2, True)
            ln(L, LW)
            finish(L - 1, True)
            finish(L, True, LW)
